import numpy as np
import ml_dtypes


def mxq(x, axis, fmt="e4m3"):
    dtype, down = {"e4m3": (ml_dtypes.float8_e4m3fn, 7), "e5m2": (ml_dtypes.float8_e5m2, 14)}[fmt]
    v = np.moveaxis(np.asarray(x, np.float32).astype(ml_dtypes.bfloat16).astype(np.float64), axis, -1)
    blocks = v.reshape(v.shape[:-1] + (-1, 32))
    amax = np.abs(blocks).max(-1, keepdims=True)
    byte = np.maximum(np.where(amax > 0, np.frexp(amax)[1] - 1 + 127, 0) - down, 1)
    scale = np.exp2(byte - 127.0)
    codes = (blocks / scale).astype(np.float32).astype(dtype).astype(np.float64)
    return np.moveaxis((codes * scale).reshape(v.shape), -1, axis)


WIDE = False


def mx_kscale(k):
    if not WIDE:
        return np.ones(k)
    levels = np.array([10, -10, 5, -5, 0])
    a = np.random.permutation(np.resize(levels, k // 512 * 4)).reshape(k // 512, 4)
    idx = np.arange(k)
    return np.exp2(a[idx // 512, idx % 128 // 32])


BF16 = ml_dtypes.bfloat16


def bf(x):
    return np.asarray(x, np.float32).astype(BF16)


def f64(x):
    return np.asarray(x).astype(np.float64)


B, D_IN, HID, F = 4096, 512, 1024, 128
L = 2 * F


def koopman_rotate(enc_x, delta_t, amplitudes, frequencies):
    n = enc_x.shape[0]
    amp = amplitudes[None, :] ** delta_t[:, None]
    ang = frequencies[None, :] * delta_t[:, None]
    c = amp * np.cos(ang)
    sn = amp * np.sin(ang)
    xe = enc_x.reshape(n, -1, 2)
    ev, od = xe[..., 0], xe[..., 1]
    out = np.stack([c * ev - sn * od, sn * ev + c * od], axis=-1)
    return out.reshape(n, -1)


def setup_inputs():
    s = mx_kscale(D_IN)
    return {
        "x": bf(np.random.standard_normal((B, D_IN)) * s),
        "delta_t": bf(np.random.uniform(0.1, 1.0, B)),
        "W_enc1": bf(np.random.standard_normal((D_IN, HID)) / np.sqrt(D_IN) / s[:, None]),
        "b_enc1": bf(np.random.standard_normal(HID) * 0.2),
        "W_enc2": bf(np.random.standard_normal((HID, L)) / np.sqrt(HID)),
        "b_enc2": bf(np.random.standard_normal(L) * 0.2),
        "amplitudes": bf(np.random.uniform(0.5, 1.5, F)),
        "frequencies": bf(np.random.uniform(0.0, 2.0 * np.pi, F)),
    }


def reference(x, delta_t, W_enc1, b_enc1, W_enc2, b_enc2, amplitudes, frequencies):
    h = np.tanh((mxq(f64(x), 1, "e4m3") @ mxq(f64(W_enc1), 0, "e4m3")) + f64(b_enc1))
    enc_x = (mxq(h, 1, "e4m3") @ mxq(f64(W_enc2), 0, "e4m3")) + f64(b_enc2)
    enc_pred = koopman_rotate(enc_x, f64(delta_t), f64(amplitudes), f64(frequencies))
    return (enc_pred, enc_x)

@@ -1,0 +1,344 @@
+import math
+from contextlib import ExitStack
+
+import concourse.mybir as mybir
+from concourse.masks import make_identity
+
+BF16 = mybir.dt.bfloat16
+F32 = mybir.dt.float32
+I32 = mybir.dt.int32
+U32 = mybir.dt.uint32
+U8 = mybir.dt.uint8
+FP8X4 = mybir.dt.float8_e4m3fn_x4
+ACT = mybir.ActivationFunctionType
+ALU = mybir.AluOpType
+
+P = 128
+PACK = 4
+ROWS, D_IN, HID, PAIRS = 4096, 512, 1024, 128
+LATENT = 2 * PAIRS
+CHUNK = 512
+TILES = CHUNK // P
+N_CHUNKS = ROWS // CHUNK
+HID_TILES = HID // P
+PASSES2 = HID // (P * PACK)
+QUADRANTS = 4
+SCALAR_ROWS = 128
+Z_BANKS = 3
+
+FLOPS = 2 * ROWS * D_IN * HID + 2 * ROWS * HID * LATENT
+
+
+def regroup(copy, grouped, planes):
+    copy(
+        out=grouped.rearrange("p (c i) t -> p c t i", i=4),
+        in_=planes.rearrange("p t (c i) -> p c t i", i=4),
+    )
+
+
+def quantise(nc, codes, scales, grouped):
+    nc.vector.quantize_mx(
+        out=codes.bitcast(FP8X4),
+        scales=scales,
+        in_=grouped.rearrange("p c t -> p (c t)"),
+    )
+
+
+def tile_koopmanae_pa_t_kernel(
+    tc, x, delta_t, W_enc1, b_enc1, W_enc2, b_enc2, amplitudes, frequencies, out_0, out_1
+):
+    nc = tc.nc
+    with ExitStack() as ctx:
+        keep = ctx.enter_context(tc.tile_pool(name="keep", bufs=1))
+        x_pool = ctx.enter_context(tc.tile_pool(name="x_pool", bufs=N_CHUNKS))
+        two = ctx.enter_context(tc.tile_pool(name="two", bufs=2))
+        three = ctx.enter_context(tc.tile_pool(name="three", bufs=3))
+        psum_z = ctx.enter_context(tc.psum_pool(name="psum_z", bufs=Z_BANKS))
+        psum_xt = ctx.enter_context(tc.psum_pool(name="psum_xt", bufs=2))
+        psum_enc = ctx.enter_context(tc.psum_pool(name="psum_enc", bufs=2))
+        psum_angle = ctx.enter_context(tc.psum_pool(name="psum_angle", bufs=1))
+        ctx.enter_context(tc.manual_schedule())
+
+        dt_rows = keep.tile([P, ROWS], BF16)
+        nc.vector.memset(dt_rows[:].bitcast(I32), 0)
+        amp_all = keep.tile([P, PAIRS], BF16)
+        nc.scalar.dma_start(out=amp_all[:], in_=amplitudes.partition_broadcast(P))
+        nc.scalar.dma_start(out=dt_rows[0:P:32, :], in_=delta_t.partition_broadcast(QUADRANTS))
+        freq_all = keep.tile([P, PAIRS], BF16)
+        nc.scalar.dma_start(out=freq_all[:], in_=frequencies.partition_broadcast(P))
+        b1_bf = keep.tile([P, HID_TILES], BF16)
+        with nc.allow_non_contiguous_dma(reason="1024 bias values, one hidden unit a partition"):
+            nc.scalar.dma_start(out=b1_bf[:], in_=b_enc1.rearrange("(m p) -> p m", p=P))
+        b2_bf = keep.tile([P, LATENT], BF16)
+        nc.scalar.dma_start(out=b2_bf[:], in_=b_enc2.partition_broadcast(P))
+
+        x_rows = x.rearrange("(c a r) k -> c r a k", a=TILES, r=P)
+        x_sb = {}
+
+        def load_x(c):
+            x_sb[c] = x_pool.tile([P, TILES, D_IN], BF16, name="x_sb")
+            nc.sync.dma_start(out=x_sb[c][:], in_=x_rows[c])
+
+        load_x(0)
+        w1_raw = keep.tile([P, PACK, HID], BF16)
+        nc.sync.dma_start(
+            out=w1_raw[:].rearrange("q (u e) c -> q u (e c)", u=2),
+            in_=W_enc1.rearrange("(u q e) c -> q u (e c)", u=2, e=2),
+        )
+        load_x(1)
+        w2_raw = keep.tile([P, HID_TILES, LATENT], BF16)
+        nc.sync.dma_start(out=w2_raw[:], in_=W_enc2.rearrange("(m p) f -> p m f", p=P))
+        for c in range(2, N_CHUNKS):
+            load_x(c)
+
+        identity = keep.tile([P, P], F32)
+        make_identity(nc, identity[:])
+
+        ln_left = keep.tile([P, PAIRS], F32)
+        nc.scalar.activation(out=ln_left[:], in_=amp_all[:], func=ACT.Ln)
+        ln_pieces = keep.tile([P, PAIRS], BF16)
+        for q in range(QUADRANTS):
+            rows = slice(32 * q, 32 * q + 32)
+            nc.vector.tensor_copy(out=ln_pieces[rows, :], in_=ln_left[rows, :])
+            if q + 1 < QUADRANTS:
+                piece = two.tile([P, PAIRS], BF16)
+                nc.vector.tensor_copy(out=piece[:], in_=ln_left[:])
+                nc.vector.tensor_sub(out=ln_left[:], in0=ln_left[:], in1=piece[:])
+
+        def outer_product(bank, c, table):
+            for a in range(TILES):
+                first = c * CHUNK + a * P
+                nc.tensor.matmul(
+                    out=bank[:, a, :],
+                    lhsT=dt_rows[:, first : first + P],
+                    rhs=table[:],
+                    start=True,
+                    stop=True,
+                )
+
+        b1_cols = keep.tile([P, HID_TILES], F32)
+        nc.vector.tensor_copy(out=b1_cols[:], in_=b1_bf[:])
+        b2_all = keep.tile([P, LATENT], F32)
+        nc.vector.tensor_copy(out=b2_all[:], in_=b2_bf[:])
+
+        w1_grouped = keep.tile([P, HID, PACK], BF16, align_bytes=64)
+        w1_codes = keep.tile([P, HID], U32, align_bytes=64)
+        w1_scales = keep.tile([P, HID], U8, align_bytes=64)
+        w2_grouped = keep.tile([P, PASSES2, LATENT, PACK], BF16, align_bytes=64)
+        w2_codes = keep.tile([P, PASSES2, LATENT], U32, align_bytes=64)
+        w2_scales = keep.tile([P, PASSES2, LATENT], U8, align_bytes=64)
+        halves = [slice(0, HID // 2), slice(HID // 2, HID)]
+        for cols in halves:
+            regroup(nc.vector.tensor_copy, w1_grouped[:, cols, :], w1_raw[:, :, cols])
+        for cols in halves:
+            quantise(nc, w1_codes[:, cols], w1_scales[:, cols], w1_grouped[:, cols, :])
+
+        def prepare_w2():
+            for g in range(PASSES2):
+                planes = w2_raw[:, PACK * g : PACK * g + PACK, :]
+                regroup(nc.vector.tensor_copy, w2_grouped[:, g], planes)
+            quantise(
+                nc,
+                w2_codes[:].rearrange("p g f -> p (g f)"),
+                w2_scales[:].rearrange("p g f -> p (g f)"),
+                w2_grouped[:].rearrange("p g f t -> p (g f) t"),
+            )
+
+        prepare_w2()
+        growth = keep.tile([P, N_CHUNKS, TILES, PAIRS], F32)
+
+        def amplitude_powers():
+            for c in range(N_CHUNKS):
+                exponent = psum_z.tile([P, TILES, PAIRS], F32, tag="z")
+                outer_product(exponent, c, ln_pieces)
+                nc.scalar.activation(out=growth[:, c], in_=exponent[:], func=ACT.Exp)
+
+        def choose_table_set():
+            table_choice = keep.tile([P, 1], F32)
+            nc.scalar.activation(out=table_choice[:], in_=ln_left[:, 0:1], func=ACT.Silu)
+
+        x_banks, x_codes, x_scales = {}, {}, {}
+        h_planes, h_codes, h_scales = {}, {}, {}
+        minus_sin, one_plus_cos, cos_grown, minus_sin_grown = {}, {}, {}, {}
+        enc_banks, enc = {}, {}
+        out_pred = out_0.rearrange("(c a r) f -> c r a f", a=TILES, r=P)
+        out_enc = out_1.rearrange("(c a r) f -> c r a f", a=TILES, r=P)
+
+        def transpose_x(c):
+            words = x_sb[c][:].bitcast(F32)
+            x_banks[c] = []
+            for half in range(2):
+                bank = psum_xt.tile([P, 2, 2, P], F32, name="x_bank")
+                for a2 in range(2):
+                    for u in range(2):
+                        nc.tensor.transpose(
+                            bank[:, u, a2, :], words[:, 2 * half + a2, P * u : P * u + P], identity[:]
+                        )
+                x_banks[c].append(bank)
+
+        def copy_x(c):
+            x_grouped = two.tile([P, CHUNK, PACK], BF16, align_bytes=64)
+            as_words = x_grouped[:].bitcast(F32)
+            for half in range(2):
+                nc.scalar.copy(
+                    out=as_words[:, 2 * P * half : 2 * P * half + 2 * P, :],
+                    in_=x_banks[c][half][:].rearrange("q u a r -> q (a r) u"),
+                )
+            return x_grouped
+
+        def quantise_x(c, x_grouped):
+            x_codes[c] = three.tile([P, CHUNK], U32, name="x_codes", align_bytes=64)
+            x_scales[c] = three.tile([P, CHUNK], U8, name="x_scales", align_bytes=64)
+            quantise(nc, x_codes[c][:], x_scales[c][:], x_grouped[:])
+
+        def hidden(c, tiles):
+            for m in tiles:
+                units = slice(P * m, P * m + P)
+                z = psum_z.tile([P, CHUNK], F32, tag="z")
+                nc.tensor.matmul_mx(
+                    out=z[:],
+                    lhsT=w1_codes[:, units].bitcast(FP8X4),
+                    lhsT_scale=w1_scales[:, units],
+                    rhs=x_codes[c][:].bitcast(FP8X4),
+                    rhs_scale=x_scales[c][:],
+                    start=True,
+                    stop=True,
+                )
+                nc.scalar.activation(
+                    out=h_planes[c][:, m, :], in_=z[:], func=ACT.Tanh, bias=b1_cols[:, m : m + 1]
+                )
+
+        def turn_functions(c):
+            angle4 = psum_angle.tile([P, TILES, PAIRS], F32)
+            outer_product(angle4, c, freq_all)
+            minus_sin[c] = three.tile([P, TILES, PAIRS], F32, name="minus_sin")
+            nc.scalar.activation(
+                out=minus_sin[c][:], in_=angle4[:], func=ACT.Sin, scale=0.25, bias=-math.pi
+            )
+            half_sin = two.tile([P, TILES, PAIRS], F32)
+            nc.scalar.activation(
+                out=half_sin[:], in_=angle4[:], func=ACT.Sin, scale=0.125, bias=-0.5 * math.pi
+            )
+            one_plus_cos[c] = three.tile([P, TILES, PAIRS], F32, name="one_plus_cos")
+            nc.scalar.activation(
+                out=one_plus_cos[c][:], in_=half_sin[:], func=ACT.Square, scale=math.sqrt(2.0)
+            )
+
+        def turn_tables(c):
+            cos_grown[c] = two.tile([P, TILES * PAIRS], F32, name="cos_grown")
+            nc.vector.scalar_tensor_tensor(
+                out=cos_grown[c][:],
+                in0=one_plus_cos[c][:].rearrange("p a i -> p (a i)"),
+                scalar=1.0,
+                in1=growth[:, c].rearrange("p a i -> p (a i)"),
+                op0=ALU.subtract,
+                op1=ALU.mult,
+            )
+            minus_sin_grown[c] = two.tile([P, TILES * PAIRS], F32, name="minus_sin_grown")
+            nc.vector.tensor_mul(
+                out=minus_sin_grown[c][:],
+                in0=minus_sin[c][:].rearrange("p a i -> p (a i)"),
+                in1=growth[:, c].rearrange("p a i -> p (a i)"),
+            )
+
+        def regroup_h(c):
+            h_grouped = two.tile([P, PASSES2, CHUNK, PACK], BF16, align_bytes=64)
+            shares = [
+                (nc.vector.tensor_copy, slice(0, CHUNK - SCALAR_ROWS)),
+                (nc.scalar.copy, slice(CHUNK - SCALAR_ROWS, CHUNK)),
+            ]
+            for copy, rows in shares:
+                for g in range(PASSES2):
+                    planes = h_planes[c][:, PACK * g : PACK * g + PACK, rows]
+                    regroup(copy, h_grouped[:, g, rows, :], planes)
+            return h_grouped
+
+        def quantise_h(c, h_grouped):
+            h_codes[c] = two.tile([P, PASSES2, CHUNK], U32, name="h_codes", align_bytes=64)
+            h_scales[c] = two.tile([P, PASSES2, CHUNK], U8, name="h_scales", align_bytes=64)
+            for g in range(PASSES2):
+                quantise(nc, h_codes[c][:, g], h_scales[c][:, g], h_grouped[:, g])
+
+        def encode(c):
+            enc_banks[c] = []
+            for half in range(2):
+                bank = psum_enc.tile([P, 2, LATENT], F32, name="enc_bank")
+                for a2 in range(2):
+                    rows = slice(P * (2 * half + a2), P * (2 * half + a2) + P)
+                    for g in range(PASSES2):
+                        nc.tensor.matmul_mx(
+                            out=bank[:, a2, :],
+                            lhsT=h_codes[c][:, g, rows].bitcast(FP8X4),
+                            lhsT_scale=h_scales[c][:, g, rows],
+                            rhs=w2_codes[:, g, :].bitcast(FP8X4),
+                            rhs_scale=w2_scales[:, g, :],
+                            start=(g == 0),
+                            stop=(g == PASSES2 - 1),
+                        )
+                enc_banks[c].append(bank)
+
+        def add_bias2(c):
+            enc[c] = three.tile([P, TILES, LATENT], F32, name="enc")
+            for half in range(2):
+                nc.vector.tensor_add(
+                    out=enc[c][:, 2 * half : 2 * half + 2, :],
+                    in0=enc_banks[c][half][:],
+                    in1=b2_all[:].unsqueeze(1).to_broadcast([P, 2, LATENT]),
+                )
+            nc.sync.dma_start(out=out_enc[c], in_=enc[c][:])
+
+        def turn(c):
+            pairs = enc[c][:].rearrange("p a (i h) -> p (a i) h", h=2)
+            n = TILES * PAIRS
+            straight = two.tile([P, n, 2], F32)
+            nc.vector.tensor_mul(
+                out=straight[:], in0=pairs, in1=cos_grown[c][:].unsqueeze(2).to_broadcast([P, n, 2])
+            )
+            crossed = two.tile([P, 2, n], F32)
+            nc.vector.tensor_mul(out=crossed[:, 0, :], in0=pairs[:, :, 1], in1=minus_sin_grown[c][:])
+            nc.vector.scalar_tensor_tensor(
+                out=crossed[:, 1, :],
+                in0=pairs[:, :, 0],
+                scalar=-1.0,
+                in1=minus_sin_grown[c][:],
+                op0=ALU.mult,
+                op1=ALU.mult,
+            )
+            pred = three.tile([P, n, 2], F32)
+            nc.vector.tensor_add(
+                out=pred[:], in0=straight[:], in1=crossed[:].rearrange("p h n -> p n h")
+            )
+            nc.sync.dma_start(
+                out=out_pred[c], in_=pred[:].rearrange("p (a i) h -> p a (i h)", a=TILES)
+            )
+
+        def live(c):
+            return 0 <= c < N_CHUNKS
+
+        def cycle(c):
+            if live(c):
+                h_planes[c] = three.tile([P, HID_TILES, CHUNK], BF16, name="h_planes")
+                hidden(c, range(0, Z_BANKS))
+            if live(c - 1):
+                encode(c - 1)
+                add_bias2(c - 1)
+                turn(c - 1)
+            if live(c):
+                hidden(c, range(Z_BANKS, HID_TILES))
+                h_grouped = regroup_h(c)
+            if live(c + 1):
+                turn_functions(c + 1)
+            if live(c + 2):
+                transpose_x(c + 2)
+                x_grouped = copy_x(c + 2)
+            if live(c):
+                quantise_h(c, h_grouped)
+                turn_tables(c)
+            if live(c + 2):
+                quantise_x(c + 2, x_grouped)
+
+        cycle(-2)
+        amplitude_powers()
+        choose_table_set()
+        for c in range(-1, N_CHUNKS + 1):
+            cycle(c)

@@ -23,8 +23,8 @@ N_CHUNKS = ROWS // CHUNK
 HID_TILES = HID // P
 PASSES2 = HID // (P * PACK)
 QUADRANTS = 4
-SCALAR_ROWS = 128
-Z_BANKS = 3
+SCALAR_ROWS = 192
+Z_BANKS = 4
 
 FLOPS = 2 * ROWS * D_IN * HID + 2 * ROWS * HID * LATENT
 
@@ -54,9 +54,8 @@ def tile_koopmanae_pa_t_kernel(
         two = ctx.enter_context(tc.tile_pool(name="two", bufs=2))
         three = ctx.enter_context(tc.tile_pool(name="three", bufs=3))
         psum_z = ctx.enter_context(tc.psum_pool(name="psum_z", bufs=Z_BANKS))
-        psum_xt = ctx.enter_context(tc.psum_pool(name="psum_xt", bufs=2))
         psum_enc = ctx.enter_context(tc.psum_pool(name="psum_enc", bufs=2))
-        psum_angle = ctx.enter_context(tc.psum_pool(name="psum_angle", bufs=1))
+        psum_small = ctx.enter_context(tc.psum_pool(name="psum_small", bufs=2))
         ctx.enter_context(tc.manual_schedule())
 
         dt_rows = keep.tile([P, ROWS], BF16)
@@ -95,15 +94,17 @@ def tile_koopmanae_pa_t_kernel(
         make_identity(nc, identity[:])
 
         ln_left = keep.tile([P, PAIRS], F32)
-        nc.scalar.activation(out=ln_left[:], in_=amp_all[:], func=ACT.Ln)
         ln_pieces = keep.tile([P, PAIRS], BF16)
-        for q in range(QUADRANTS):
-            rows = slice(32 * q, 32 * q + 32)
-            nc.vector.tensor_copy(out=ln_pieces[rows, :], in_=ln_left[rows, :])
-            if q + 1 < QUADRANTS:
-                piece = two.tile([P, PAIRS], BF16)
-                nc.vector.tensor_copy(out=piece[:], in_=ln_left[:])
-                nc.vector.tensor_sub(out=ln_left[:], in0=ln_left[:], in1=piece[:])
+
+        def split_ln_amplitudes():
+            nc.scalar.activation(out=ln_left[:], in_=amp_all[:], func=ACT.Ln)
+            for q in range(QUADRANTS):
+                rows = slice(32 * q, 32 * q + 32)
+                nc.vector.tensor_copy(out=ln_pieces[rows, :], in_=ln_left[rows, :])
+                if q + 1 < QUADRANTS:
+                    piece = two.tile([P, PAIRS], BF16)
+                    nc.vector.tensor_copy(out=piece[:], in_=ln_left[:])
+                    nc.vector.tensor_sub(out=ln_left[:], in0=ln_left[:], in1=piece[:])
 
         def outer_product(bank, c, table):
             for a in range(TILES):
@@ -116,35 +117,6 @@ def tile_koopmanae_pa_t_kernel(
                     stop=True,
                 )
 
-        b1_cols = keep.tile([P, HID_TILES], F32)
-        nc.vector.tensor_copy(out=b1_cols[:], in_=b1_bf[:])
-        b2_all = keep.tile([P, LATENT], F32)
-        nc.vector.tensor_copy(out=b2_all[:], in_=b2_bf[:])
-
-        w1_grouped = keep.tile([P, HID, PACK], BF16, align_bytes=64)
-        w1_codes = keep.tile([P, HID], U32, align_bytes=64)
-        w1_scales = keep.tile([P, HID], U8, align_bytes=64)
-        w2_grouped = keep.tile([P, PASSES2, LATENT, PACK], BF16, align_bytes=64)
-        w2_codes = keep.tile([P, PASSES2, LATENT], U32, align_bytes=64)
-        w2_scales = keep.tile([P, PASSES2, LATENT], U8, align_bytes=64)
-        halves = [slice(0, HID // 2), slice(HID // 2, HID)]
-        for cols in halves:
-            regroup(nc.vector.tensor_copy, w1_grouped[:, cols, :], w1_raw[:, :, cols])
-        for cols in halves:
-            quantise(nc, w1_codes[:, cols], w1_scales[:, cols], w1_grouped[:, cols, :])
-
-        def prepare_w2():
-            for g in range(PASSES2):
-                planes = w2_raw[:, PACK * g : PACK * g + PACK, :]
-                regroup(nc.vector.tensor_copy, w2_grouped[:, g], planes)
-            quantise(
-                nc,
-                w2_codes[:].rearrange("p g f -> p (g f)"),
-                w2_scales[:].rearrange("p g f -> p (g f)"),
-                w2_grouped[:].rearrange("p g f t -> p (g f) t"),
-            )
-
-        prepare_w2()
         growth = keep.tile([P, N_CHUNKS, TILES, PAIRS], F32)
 
         def amplitude_powers():
@@ -157,39 +129,73 @@ def tile_koopmanae_pa_t_kernel(
             table_choice = keep.tile([P, 1], F32)
             nc.scalar.activation(out=table_choice[:], in_=ln_left[:, 0:1], func=ACT.Silu)
 
-        x_banks, x_codes, x_scales = {}, {}, {}
-        h_planes, h_codes, h_scales = {}, {}, {}
-        minus_sin, one_plus_cos, cos_grown, minus_sin_grown = {}, {}, {}, {}
+        b1_cols = keep.tile([P, HID_TILES], F32)
+        b2_all = keep.tile([P, LATENT], F32)
+
+        def widen_biases():
+            nc.vector.tensor_copy(out=b1_cols[:], in_=b1_bf[:])
+            nc.vector.tensor_copy(out=b2_all[:], in_=b2_bf[:])
+
+        w1_grouped = keep.tile([P, HID, PACK], BF16, align_bytes=64)
+        w1_codes = keep.tile([P, HID], U32, align_bytes=64)
+        w1_scales = keep.tile([P, HID], U8, align_bytes=64)
+        w1_halves = [slice(0, HID // 2), slice(HID // 2, HID)]
+
+        def regroup_w1():
+            for cols in w1_halves:
+                regroup(nc.vector.tensor_copy, w1_grouped[:, cols, :], w1_raw[:, :, cols])
+
+        def quantise_w1():
+            for cols in w1_halves:
+                quantise(nc, w1_codes[:, cols], w1_scales[:, cols], w1_grouped[:, cols, :])
+
+        w2_grouped = keep.tile([P, PASSES2, LATENT, PACK], BF16, align_bytes=64)
+        w2_codes = keep.tile([P, PASSES2, LATENT], U32, align_bytes=64)
+        w2_scales = keep.tile([P, PASSES2, LATENT], U8, align_bytes=64)
+
+        def regroup_w2():
+            for g in range(PASSES2):
+                planes = w2_raw[:, PACK * g : PACK * g + PACK, :]
+                regroup(nc.vector.tensor_copy, w2_grouped[:, g], planes)
+
+        def quantise_w2():
+            quantise(
+                nc,
+                w2_codes[:].rearrange("p g f -> p (g f)"),
+                w2_scales[:].rearrange("p g f -> p (g f)"),
+                w2_grouped[:].rearrange("p g f t -> p (g f) t"),
+            )
+
+        x_banks, x_grouped, x_codes, x_scales = {}, {}, {}, {}
+        h_planes, h_grouped, h_codes, h_scales = {}, {}, {}, {}
+        minus_sin, half_sin, one_plus_cos, cos_grown, minus_sin_grown = {}, {}, {}, {}, {}
         enc_banks, enc = {}, {}
         out_pred = out_0.rearrange("(c a r) f -> c r a f", a=TILES, r=P)
         out_enc = out_1.rearrange("(c a r) f -> c r a f", a=TILES, r=P)
 
-        def transpose_x(c):
+        def transpose_x(c, half):
             words = x_sb[c][:].bitcast(F32)
-            x_banks[c] = []
-            for half in range(2):
-                bank = psum_xt.tile([P, 2, 2, P], F32, name="x_bank")
-                for a2 in range(2):
-                    for u in range(2):
-                        nc.tensor.transpose(
-                            bank[:, u, a2, :], words[:, 2 * half + a2, P * u : P * u + P], identity[:]
-                        )
-                x_banks[c].append(bank)
+            bank = psum_small.tile([P, 2, 2, P], F32, tag="small")
+            for a2 in range(2):
+                for u in range(2):
+                    nc.tensor.transpose(
+                        bank[:, u, a2, :], words[:, 2 * half + a2, P * u : P * u + P], identity[:]
+                    )
+            x_banks[c, half] = bank
 
-        def copy_x(c):
-            x_grouped = two.tile([P, CHUNK, PACK], BF16, align_bytes=64)
-            as_words = x_grouped[:].bitcast(F32)
-            for half in range(2):
-                nc.scalar.copy(
-                    out=as_words[:, 2 * P * half : 2 * P * half + 2 * P, :],
-                    in_=x_banks[c][half][:].rearrange("q u a r -> q (a r) u"),
-                )
-            return x_grouped
+        def copy_x(c, half, copy):
+            if half == 0:
+                x_grouped[c] = two.tile([P, CHUNK, PACK], BF16, name="x_grouped", align_bytes=64)
+            as_words = x_grouped[c][:].bitcast(F32)
+            copy(
+                out=as_words[:, 2 * P * half : 2 * P * half + 2 * P, :],
+                in_=x_banks[c, half][:].rearrange("q u a r -> q (a r) u"),
+            )
 
-        def quantise_x(c, x_grouped):
+        def quantise_x(c):
             x_codes[c] = three.tile([P, CHUNK], U32, name="x_codes", align_bytes=64)
             x_scales[c] = three.tile([P, CHUNK], U8, name="x_scales", align_bytes=64)
-            quantise(nc, x_codes[c][:], x_scales[c][:], x_grouped[:])
+            quantise(nc, x_codes[c][:], x_scales[c][:], x_grouped[c][:])
 
         def hidden(c, tiles):
             for m in tiles:
@@ -208,20 +214,22 @@ def tile_koopmanae_pa_t_kernel(
                     out=h_planes[c][:, m, :], in_=z[:], func=ACT.Tanh, bias=b1_cols[:, m : m + 1]
                 )
 
-        def turn_functions(c):
-            angle4 = psum_angle.tile([P, TILES, PAIRS], F32)
+        def sines(c):
+            angle4 = psum_small.tile([P, TILES, PAIRS], F32, tag="small")
             outer_product(angle4, c, freq_all)
             minus_sin[c] = three.tile([P, TILES, PAIRS], F32, name="minus_sin")
             nc.scalar.activation(
                 out=minus_sin[c][:], in_=angle4[:], func=ACT.Sin, scale=0.25, bias=-math.pi
             )
-            half_sin = two.tile([P, TILES, PAIRS], F32)
+            half_sin[c] = two.tile([P, TILES, PAIRS], F32, name="half_sin")
             nc.scalar.activation(
-                out=half_sin[:], in_=angle4[:], func=ACT.Sin, scale=0.125, bias=-0.5 * math.pi
+                out=half_sin[c][:], in_=angle4[:], func=ACT.Sin, scale=0.125, bias=-0.5 * math.pi
             )
+
+        def cosine(c):
             one_plus_cos[c] = three.tile([P, TILES, PAIRS], F32, name="one_plus_cos")
             nc.scalar.activation(
-                out=one_plus_cos[c][:], in_=half_sin[:], func=ACT.Square, scale=math.sqrt(2.0)
+                out=one_plus_cos[c][:], in_=half_sin[c][:], func=ACT.Square, scale=math.sqrt(2.0)
             )
 
         def turn_tables(c):
@@ -241,26 +249,18 @@ def tile_koopmanae_pa_t_kernel(
                 in1=growth[:, c].rearrange("p a i -> p (a i)"),
             )
 
-        def regroup_h(c):
-            h_grouped = two.tile([P, PASSES2, CHUNK, PACK], BF16, align_bytes=64)
-            shares = [
-                (nc.vector.tensor_copy, slice(0, CHUNK - SCALAR_ROWS)),
-                (nc.scalar.copy, slice(CHUNK - SCALAR_ROWS, CHUNK)),
-            ]
-            for copy, rows in shares:
-                for g in range(PASSES2):
-                    planes = h_planes[c][:, PACK * g : PACK * g + PACK, rows]
-                    regroup(copy, h_grouped[:, g, rows, :], planes)
-            return h_grouped
+        def regroup_h(c, copy, rows):
+            for g in range(PASSES2):
+                planes = h_planes[c][:, PACK * g : PACK * g + PACK, rows]
+                regroup(copy, h_grouped[c][:, g, rows, :], planes)
 
-        def quantise_h(c, h_grouped):
+        def quantise_h(c):
             h_codes[c] = two.tile([P, PASSES2, CHUNK], U32, name="h_codes", align_bytes=64)
             h_scales[c] = two.tile([P, PASSES2, CHUNK], U8, name="h_scales", align_bytes=64)
             for g in range(PASSES2):
-                quantise(nc, h_codes[c][:, g], h_scales[c][:, g], h_grouped[:, g])
+                quantise(nc, h_codes[c][:, g], h_scales[c][:, g], h_grouped[c][:, g])
 
         def encode(c):
-            enc_banks[c] = []
             for half in range(2):
                 bank = psum_enc.tile([P, 2, LATENT], F32, name="enc_bank")
                 for a2 in range(2):
@@ -275,14 +275,14 @@ def tile_koopmanae_pa_t_kernel(
                             start=(g == 0),
                             stop=(g == PASSES2 - 1),
                         )
-                enc_banks[c].append(bank)
+                enc_banks[c, half] = bank
 
         def add_bias2(c):
             enc[c] = three.tile([P, TILES, LATENT], F32, name="enc")
             for half in range(2):
                 nc.vector.tensor_add(
                     out=enc[c][:, 2 * half : 2 * half + 2, :],
-                    in0=enc_banks[c][half][:],
+                    in0=enc_banks[c, half][:],
                     in1=b2_all[:].unsqueeze(1).to_broadcast([P, 2, LATENT]),
                 )
             nc.sync.dma_start(out=out_enc[c], in_=enc[c][:])
@@ -312,10 +312,32 @@ def tile_koopmanae_pa_t_kernel(
                 out=out_pred[c], in_=pred[:].rearrange("p (a i) h -> p a (i h)", a=TILES)
             )
 
+        split_ln_amplitudes()
+        transpose_x(0, 0)
+        transpose_x(0, 1)
+        amplitude_powers()
+        choose_table_set()
+        copy_x(0, 0, nc.vector.tensor_copy)
+        copy_x(0, 1, nc.vector.tensor_copy)
+        widen_biases()
+        regroup_w1()
+        quantise_x(0)
+        quantise_w1()
+        transpose_x(1, 0)
+        transpose_x(1, 1)
+        copy_x(1, 0, nc.vector.tensor_copy)
+        copy_x(1, 1, nc.vector.tensor_copy)
+        regroup_w2()
+        quantise_x(1)
+        quantise_w2()
+
+        vector_rows = slice(0, CHUNK - SCALAR_ROWS)
+        scalar_rows = slice(CHUNK - SCALAR_ROWS, CHUNK)
+
         def live(c):
             return 0 <= c < N_CHUNKS
 
-        def cycle(c):
+        for c in range(N_CHUNKS + 1):
             if live(c):
                 h_planes[c] = three.tile([P, HID_TILES, CHUNK], BF16, name="h_planes")
                 hidden(c, range(0, Z_BANKS))
@@ -325,20 +347,22 @@ def tile_koopmanae_pa_t_kernel(
                 turn(c - 1)
             if live(c):
                 hidden(c, range(Z_BANKS, HID_TILES))
-                h_grouped = regroup_h(c)
-            if live(c + 1):
-                turn_functions(c + 1)
+                h_grouped[c] = two.tile(
+                    [P, PASSES2, CHUNK, PACK], BF16, name="h_grouped", align_bytes=64
+                )
+                regroup_h(c, nc.vector.tensor_copy, vector_rows)
+                sines(c)
             if live(c + 2):
-                transpose_x(c + 2)
-                x_grouped = copy_x(c + 2)
+                transpose_x(c + 2, 0)
             if live(c):
-                quantise_h(c, h_grouped)
+                regroup_h(c, nc.scalar.copy, scalar_rows)
+                cosine(c)
+            if live(c + 2):
+                transpose_x(c + 2, 1)
+                copy_x(c + 2, 0, nc.scalar.copy)
+                copy_x(c + 2, 1, nc.scalar.copy)
+            if live(c):
+                quantise_h(c)
                 turn_tables(c)
             if live(c + 2):
-                quantise_x(c + 2, x_grouped)
-
-        cycle(-2)
-        amplitude_powers()
-        choose_table_set()
-        for c in range(-1, N_CHUNKS + 1):
-            cycle(c)
+                quantise_x(c + 2)

@@ -23,6 +23,7 @@ N_CHUNKS = ROWS // CHUNK
 HID_TILES = HID // P
 PASSES2 = HID // (P * PACK)
 QUADRANTS = 4
+LN_PIECES = 3
 SCALAR_ROWS = 192
 Z_BANKS = 4
 
@@ -95,13 +96,14 @@ def tile_koopmanae_pa_t_kernel(
 
         ln_left = keep.tile([P, PAIRS], F32)
         ln_pieces = keep.tile([P, PAIRS], BF16)
+        nc.vector.memset(ln_pieces[:], 0.0)
 
         def split_ln_amplitudes():
             nc.scalar.activation(out=ln_left[:], in_=amp_all[:], func=ACT.Ln)
-            for q in range(QUADRANTS):
+            for q in range(LN_PIECES):
                 rows = slice(32 * q, 32 * q + 32)
                 nc.vector.tensor_copy(out=ln_pieces[rows, :], in_=ln_left[rows, :])
-                if q + 1 < QUADRANTS:
+                if q + 1 < LN_PIECES:
                     piece = two.tile([P, PAIRS], BF16)
                     nc.vector.tensor_copy(out=piece[:], in_=ln_left[:])
                     nc.vector.tensor_sub(out=ln_left[:], in0=ln_left[:], in1=piece[:])
@@ -168,8 +170,8 @@ def tile_koopmanae_pa_t_kernel(
 
         x_banks, x_grouped, x_codes, x_scales = {}, {}, {}, {}
         h_planes, h_grouped, h_codes, h_scales = {}, {}, {}, {}
-        minus_sin, half_sin, one_plus_cos, cos_grown, minus_sin_grown = {}, {}, {}, {}, {}
-        enc_banks, enc = {}, {}
+        turn_functions, distance, turn_factors = {}, {}, {}
+        enc_banks, enc, straight, crossed = {}, {}, {}, {}
         out_pred = out_0.rearrange("(c a r) f -> c r a f", a=TILES, r=P)
         out_enc = out_1.rearrange("(c a r) f -> c r a f", a=TILES, r=P)
 
@@ -214,45 +216,35 @@ def tile_koopmanae_pa_t_kernel(
                     out=h_planes[c][:, m, :], in_=z[:], func=ACT.Tanh, bias=b1_cols[:, m : m + 1]
                 )
 
-        def sines(c):
+        def sine(c):
             angle4 = psum_small.tile([P, TILES, PAIRS], F32, tag="small")
             outer_product(angle4, c, freq_all)
-            minus_sin[c] = three.tile([P, TILES, PAIRS], F32, name="minus_sin")
+            turn_functions[c] = three.tile([P, 2, TILES, PAIRS], F32, name="turn_functions")
             nc.scalar.activation(
-                out=minus_sin[c][:], in_=angle4[:], func=ACT.Sin, scale=0.25, bias=-math.pi
+                out=turn_functions[c][:, 1], in_=angle4[:], func=ACT.Sin, scale=0.25, bias=-math.pi
             )
-            half_sin[c] = two.tile([P, TILES, PAIRS], F32, name="half_sin")
+            distance[c] = two.tile([P, TILES, PAIRS], F32, name="distance")
             nc.scalar.activation(
-                out=half_sin[c][:], in_=angle4[:], func=ACT.Sin, scale=0.125, bias=-0.5 * math.pi
+                out=distance[c][:], in_=angle4[:], func=ACT.Abs, scale=0.25, bias=-math.pi
             )
 
         def cosine(c):
-            one_plus_cos[c] = three.tile([P, TILES, PAIRS], F32, name="one_plus_cos")
             nc.scalar.activation(
-                out=one_plus_cos[c][:], in_=half_sin[c][:], func=ACT.Square, scale=math.sqrt(2.0)
+                out=turn_functions[c][:, 0], in_=distance[c][:], func=ACT.Sin, bias=-0.5 * math.pi
             )
 
-        def turn_tables(c):
-            cos_grown[c] = two.tile([P, TILES * PAIRS], F32, name="cos_grown")
-            nc.vector.scalar_tensor_tensor(
-                out=cos_grown[c][:],
-                in0=one_plus_cos[c][:].rearrange("p a i -> p (a i)"),
-                scalar=1.0,
-                in1=growth[:, c].rearrange("p a i -> p (a i)"),
-                op0=ALU.subtract,
-                op1=ALU.mult,
-            )
-            minus_sin_grown[c] = two.tile([P, TILES * PAIRS], F32, name="minus_sin_grown")
+        def grow(c):
+            n = TILES * PAIRS
+            turn_factors[c] = two.tile([P, 2, n], F32, name="turn_factors")
             nc.vector.tensor_mul(
-                out=minus_sin_grown[c][:],
-                in0=minus_sin[c][:].rearrange("p a i -> p (a i)"),
-                in1=growth[:, c].rearrange("p a i -> p (a i)"),
+                out=turn_factors[c][:],
+                in0=turn_functions[c][:].rearrange("p s a i -> p s (a i)"),
+                in1=growth[:, c].rearrange("p a i -> p (a i)").unsqueeze(1).to_broadcast([P, 2, n]),
             )
 
-        def regroup_h(c, copy, rows):
-            for g in range(PASSES2):
-                planes = h_planes[c][:, PACK * g : PACK * g + PACK, rows]
-                regroup(copy, h_grouped[c][:, g, rows, :], planes)
+        def regroup_h(c, g, copy, rows):
+            planes = h_planes[c][:, PACK * g : PACK * g + PACK, rows]
+            regroup(copy, h_grouped[c][:, g, rows, :], planes)
 
         def quantise_h(c):
             h_codes[c] = two.tile([P, PASSES2, CHUNK], U32, name="h_codes", align_bytes=64)
@@ -287,26 +279,32 @@ def tile_koopmanae_pa_t_kernel(
                 )
             nc.sync.dma_start(out=out_enc[c], in_=enc[c][:])
 
-        def turn(c):
-            pairs = enc[c][:].rearrange("p a (i h) -> p (a i) h", h=2)
+        def turn_products(c):
             n = TILES * PAIRS
-            straight = two.tile([P, n, 2], F32)
-            nc.vector.tensor_mul(
-                out=straight[:], in0=pairs, in1=cos_grown[c][:].unsqueeze(2).to_broadcast([P, n, 2])
-            )
-            crossed = two.tile([P, 2, n], F32)
-            nc.vector.tensor_mul(out=crossed[:, 0, :], in0=pairs[:, :, 1], in1=minus_sin_grown[c][:])
+            pairs = enc[c][:].rearrange("p a (i h) -> p (a i) h", h=2)
+            cos_grown, minus_sin_grown = turn_factors[c][:, 0, :], turn_factors[c][:, 1, :]
+            straight[c] = two.tile([P, n, 2], F32, name="straight")
+            for half in (slice(0, n // 2), slice(n // 2, n)):
+                nc.vector.tensor_mul(
+                    out=straight[c][:, half, :],
+                    in0=pairs[:, half, :],
+                    in1=cos_grown[:, half].unsqueeze(2).to_broadcast([P, n // 2, 2]),
+                )
+            crossed[c] = two.tile([P, 2, n], F32, name="crossed")
+            nc.vector.tensor_mul(out=crossed[c][:, 0, :], in0=pairs[:, :, 1], in1=minus_sin_grown)
             nc.vector.scalar_tensor_tensor(
-                out=crossed[:, 1, :],
+                out=crossed[c][:, 1, :],
                 in0=pairs[:, :, 0],
                 scalar=-1.0,
-                in1=minus_sin_grown[c][:],
+                in1=minus_sin_grown,
                 op0=ALU.mult,
                 op1=ALU.mult,
             )
-            pred = three.tile([P, n, 2], F32)
+
+        def turn_sum(c):
+            pred = three.tile([P, TILES * PAIRS, 2], F32)
             nc.vector.tensor_add(
-                out=pred[:], in0=straight[:], in1=crossed[:].rearrange("p h n -> p n h")
+                out=pred[:], in0=straight[c][:], in1=crossed[c][:].rearrange("p h n -> p n h")
             )
             nc.sync.dma_start(
                 out=out_pred[c], in_=pred[:].rearrange("p (a i) h -> p a (i h)", a=TILES)
@@ -344,18 +342,23 @@ def tile_koopmanae_pa_t_kernel(
             if live(c - 1):
                 encode(c - 1)
                 add_bias2(c - 1)
-                turn(c - 1)
+                turn_products(c - 1)
             if live(c):
                 hidden(c, range(Z_BANKS, HID_TILES))
                 h_grouped[c] = two.tile(
                     [P, PASSES2, CHUNK, PACK], BF16, name="h_grouped", align_bytes=64
                 )
-                regroup_h(c, nc.vector.tensor_copy, vector_rows)
-                sines(c)
+                regroup_h(c, 0, nc.vector.tensor_copy, vector_rows)
+            if live(c - 1):
+                turn_sum(c - 1)
+            if live(c):
+                regroup_h(c, 1, nc.vector.tensor_copy, vector_rows)
+                sine(c)
             if live(c + 2):
                 transpose_x(c + 2, 0)
             if live(c):
-                regroup_h(c, nc.scalar.copy, scalar_rows)
+                regroup_h(c, 0, nc.scalar.copy, scalar_rows)
+                regroup_h(c, 1, nc.scalar.copy, scalar_rows)
                 cosine(c)
             if live(c + 2):
                 transpose_x(c + 2, 1)
@@ -363,6 +366,6 @@ def tile_koopmanae_pa_t_kernel(
                 copy_x(c + 2, 1, nc.scalar.copy)
             if live(c):
                 quantise_h(c)
-                turn_tables(c)
+                grow(c)
             if live(c + 2):
                 quantise_x(c + 2)

@@ -1,4 +1,3 @@
-import math
 from contextlib import ExitStack
 
 import concourse.mybir as mybir
@@ -19,12 +18,15 @@ ROWS, D_IN, HID, PAIRS = 4096, 512, 1024, 128
 LATENT = 2 * PAIRS
 CHUNK = 512
 TILES = CHUNK // P
-N_CHUNKS = ROWS // CHUNK
+ROW_TILES = ROWS // P
+CHUNK_TILES = [TILES // 2] + [TILES] * (ROW_TILES // TILES - 1) + [TILES // 2]
+N_CHUNKS = len(CHUNK_TILES)
+FIRST_TILE = [sum(CHUNK_TILES[:c]) for c in range(N_CHUNKS)]
 HID_TILES = HID // P
 PASSES2 = HID // (P * PACK)
-QUADRANTS = 4
-LN_PIECES = 3
-SCALAR_ROWS = 192
+TERMS = 32
+ROW_AMP, ROW_FREQ, ROW_B1, ROW_B2, VEC_ROWS = 32, 33, 34, 42, 44
+SCALAR_WORDS = 384
 Z_BANKS = 4
 
 FLOPS = 2 * ROWS * D_IN * HID + 2 * ROWS * HID * LATENT
@@ -56,35 +58,42 @@ def tile_koopmanae_pa_t_kernel(
         three = ctx.enter_context(tc.tile_pool(name="three", bufs=3))
         psum_z = ctx.enter_context(tc.psum_pool(name="psum_z", bufs=Z_BANKS))
         psum_enc = ctx.enter_context(tc.psum_pool(name="psum_enc", bufs=2))
-        psum_small = ctx.enter_context(tc.psum_pool(name="psum_small", bufs=2))
+        psum_turn = ctx.enter_context(tc.psum_pool(name="psum_turn", bufs=1))
         ctx.enter_context(tc.manual_schedule())
 
-        dt_rows = keep.tile([P, ROWS], BF16)
-        nc.vector.memset(dt_rows[:].bitcast(I32), 0)
-        amp_all = keep.tile([P, PAIRS], BF16)
-        nc.scalar.dma_start(out=amp_all[:], in_=amplitudes.partition_broadcast(P))
-        nc.scalar.dma_start(out=dt_rows[0:P:32, :], in_=delta_t.partition_broadcast(QUADRANTS))
-        freq_all = keep.tile([P, PAIRS], BF16)
-        nc.scalar.dma_start(out=freq_all[:], in_=frequencies.partition_broadcast(P))
-        b1_bf = keep.tile([P, HID_TILES], BF16)
-        with nc.allow_non_contiguous_dma(reason="1024 bias values, one hidden unit a partition"):
-            nc.scalar.dma_start(out=b1_bf[:], in_=b_enc1.rearrange("(m p) -> p m", p=P))
-        b2_bf = keep.tile([P, LATENT], BF16)
-        nc.scalar.dma_start(out=b2_bf[:], in_=b_enc2.partition_broadcast(P))
+        vec = keep.tile([P, P], BF16)
+        nc.vector.memset(vec[:].bitcast(I32), 0)
+        nc.sync.dma_start(out=vec[0:ROW_AMP, :], in_=delta_t.rearrange("(t r) -> t r", r=P))
+        nc.sync.dma_start(
+            out=vec[ROW_AMP:ROW_FREQ, :], in_=amplitudes.rearrange("(o i) -> o i", o=1)
+        )
+        nc.sync.dma_start(
+            out=vec[ROW_FREQ:ROW_B1, :], in_=frequencies.rearrange("(o i) -> o i", o=1)
+        )
+        nc.sync.dma_start(out=vec[ROW_B1:ROW_B2, :], in_=b_enc1.rearrange("(m p) -> m p", p=P))
+        nc.sync.dma_start(out=vec[ROW_B2:VEC_ROWS, :], in_=b_enc2.rearrange("(m p) -> m p", p=P))
 
-        x_rows = x.rearrange("(c a r) k -> c r a k", a=TILES, r=P)
+        def rows_of(c):
+            return slice(P * FIRST_TILE[c], P * (FIRST_TILE[c] + CHUNK_TILES[c]))
+
         x_sb = {}
 
         def load_x(c):
             x_sb[c] = x_pool.tile([P, TILES, D_IN], BF16, name="x_sb")
-            nc.sync.dma_start(out=x_sb[c][:], in_=x_rows[c])
+            nc.sync.dma_start(
+                out=x_sb[c][:, 0 : CHUNK_TILES[c], :],
+                in_=x[rows_of(c), :].rearrange("(a r) k -> r a k", r=P),
+            )
 
         load_x(0)
-        w1_raw = keep.tile([P, PACK, HID], BF16)
-        nc.sync.dma_start(
-            out=w1_raw[:].rearrange("q (u e) c -> q u (e c)", u=2),
-            in_=W_enc1.rearrange("(u q e) c -> q u (e c)", u=2, e=2),
-        )
+        W1_HALVES = [slice(0, HID // 2), slice(HID // 2, HID)]
+        w1_rows = W_enc1.rearrange("(u q e) c -> q u e c", u=2, e=2)
+        w1_raw = []
+        for half, cols in enumerate(W1_HALVES):
+            raw = keep.tile([P, PACK, HID // 2], BF16, name="w1_raw_%d" % half)
+            for u in range(2):
+                nc.sync.dma_start(out=raw[:, 2 * u : 2 * u + 2, :], in_=w1_rows[:, u, :, cols])
+            w1_raw.append(raw)
         load_x(1)
         w2_raw = keep.tile([P, HID_TILES, LATENT], BF16)
         nc.sync.dma_start(out=w2_raw[:], in_=W_enc2.rearrange("(m p) f -> p m f", p=P))
@@ -93,63 +102,145 @@ def tile_koopmanae_pa_t_kernel(
 
         identity = keep.tile([P, P], F32)
         make_identity(nc, identity[:])
+        identity_bf = keep.tile([P, P], BF16)
+        nc.gpsimd.tensor_copy(out=identity_bf[:], in_=identity[:])
 
-        ln_left = keep.tile([P, PAIRS], F32)
-        ln_pieces = keep.tile([P, PAIRS], BF16)
-        nc.vector.memset(ln_pieces[:], 0.0)
+        first = keep.tile([P, 1], F32)
+        nc.vector.memset(first[:], 1.0)
+        table_choice = keep.tile([P, 1], F32)
+        nc.scalar.activation(out=table_choice[:], in_=first[:], func=ACT.Ln)
 
-        def split_ln_amplitudes():
-            nc.scalar.activation(out=ln_left[:], in_=amp_all[:], func=ACT.Ln)
-            for q in range(LN_PIECES):
-                rows = slice(32 * q, 32 * q + 32)
-                nc.vector.tensor_copy(out=ln_pieces[rows, :], in_=ln_left[rows, :])
-                if q + 1 < LN_PIECES:
-                    piece = two.tile([P, PAIRS], BF16)
-                    nc.vector.tensor_copy(out=piece[:], in_=ln_left[:])
-                    nc.vector.tensor_sub(out=ln_left[:], in0=ln_left[:], in1=piece[:])
+        coef = keep.tile([P, 2, 4, TERMS], F32)
+        blocks = keep.tile([P, 2, TILES, PAIRS], F32)
+        nc.gpsimd.memset(blocks[:], 0.0)
+        zpow = keep.tile([P, 2, TERMS], F32)
+        nc.gpsimd.memset(zpow[:, 0, 0:1], 1.0)
+        nc.gpsimd.memset(zpow[:, 1, 0:1], 0.0)
+        tpow = keep.tile([P, ROW_TILES, TERMS], F32)
+        nc.gpsimd.memset(tpow[:, :, 0:1], 1.0)
+        counts = keep.tile([P, TERMS - 1], F32)
+        nc.gpsimd.iota(
+            counts[:],
+            pattern=[[1, TERMS - 1]],
+            base=1,
+            channel_multiplier=0,
+            allow_small_or_imprecise_dtypes=True,
+        )
+        inverses = keep.tile([P, TERMS - 1], F32)
+        zeros = keep.tile([P, TERMS - 1], F32)
+        inv_fact = keep.tile([P, TERMS], F32)
 
-        def outer_product(bank, c, table):
-            for a in range(TILES):
-                first = c * CHUNK + a * P
+        def inverse_factorials():
+            nc.vector.memset(zeros[:], 0.0)
+            nc.vector.memset(inv_fact[:, 0:1], 1.0)
+            nc.vector.reciprocal(out=inverses[:], in_=counts[:])
+            nc.vector.tensor_tensor_scan(
+                out=inv_fact[:, 1:TERMS],
+                data0=inverses[:],
+                data1=zeros[:],
+                initial=1.0,
+                op0=ALU.mult,
+                op1=ALU.add,
+            )
+
+        columns = keep.tile([P, VEC_ROWS], F32)
+        b2_all = keep.tile([P, LATENT], F32)
+
+        def spread_vectors():
+            turned = psum_z.tile([P, P], BF16, tag="z")
+            nc.tensor.transpose(turned[:], vec[:], identity_bf[:])
+            nc.vector.tensor_copy(out=columns[:], in_=turned[:, 0:VEC_ROWS])
+            spread = psum_z.tile([P, LATENT], F32, tag="z")
+            for m in range(2):
+                row = ROW_B2 + m
                 nc.tensor.matmul(
-                    out=bank[:, a, :],
-                    lhsT=dt_rows[:, first : first + P],
-                    rhs=table[:],
+                    out=spread[:, P * m : P * m + P],
+                    lhsT=identity_bf[:, row : row + 1].to_broadcast([P, P]),
+                    rhs=vec[:],
                     start=True,
                     stop=True,
                 )
+            return spread
 
-        growth = keep.tile([P, N_CHUNKS, TILES, PAIRS], F32)
+        def coefficients():
+            nc.scalar.activation(
+                out=zpow[:, 0, 1:2], in_=columns[:, ROW_AMP:ROW_FREQ], func=ACT.Ln
+            )
+            nc.gpsimd.tensor_copy(out=zpow[:, 1, 1:2], in_=columns[:, ROW_FREQ:ROW_B1])
+            by_re = keep.tile([P, 2, TERMS // 2], F32)
+            by_im = keep.tile([P, 2, TERMS // 2], F32)
+            m = 1
+            while m < TERMS - 1:
+                n = min(m, TERMS - 1 - m)
+                for part, scaled in ((0, by_re), (1, by_im)):
+                    nc.gpsimd.tensor_scalar(
+                        out=scaled[:, :, 0:n],
+                        in0=zpow[:, :, 1 : 1 + n],
+                        scalar1=zpow[:, part, m : m + 1],
+                        scalar2=0.0,
+                        op0=ALU.mult,
+                        op1=ALU.add,
+                    )
+                nc.gpsimd.tensor_sub(
+                    out=zpow[:, 0, m + 1 : m + 1 + n], in0=by_re[:, 0, 0:n], in1=by_im[:, 1, 0:n]
+                )
+                nc.gpsimd.tensor_add(
+                    out=zpow[:, 1, m + 1 : m + 1 + n], in0=by_re[:, 1, 0:n], in1=by_im[:, 0, 0:n]
+                )
+                m = 2 * m
+            for part in range(2):
+                nc.gpsimd.tensor_mul(
+                    out=coef[:, part],
+                    in0=zpow[:, part, :].unsqueeze(1).to_broadcast([P, 4, TERMS]),
+                    in1=inv_fact[:].unsqueeze(1).to_broadcast([P, 4, TERMS]),
+                )
 
-        def amplitude_powers():
-            for c in range(N_CHUNKS):
-                exponent = psum_z.tile([P, TILES, PAIRS], F32, tag="z")
-                outer_product(exponent, c, ln_pieces)
-                nc.scalar.activation(out=growth[:, c], in_=exponent[:], func=ACT.Exp)
+        def powers():
+            nc.gpsimd.tensor_copy(out=tpow[:, :, 1:2], in_=columns[:, 0:ROW_AMP].unsqueeze(2))
+            m = 1
+            while m < TERMS - 1:
+                n = min(m, TERMS - 1 - m)
+                nc.gpsimd.tensor_mul(
+                    out=tpow[:, :, m + 1 : m + 1 + n],
+                    in0=tpow[:, :, 1 : 1 + n],
+                    in1=tpow[:, :, m : m + 1].to_broadcast([P, ROW_TILES, n]),
+                )
+                m = 2 * m
 
-        def choose_table_set():
-            table_choice = keep.tile([P, 1], F32)
-            nc.scalar.activation(out=table_choice[:], in_=ln_left[:, 0:1], func=ACT.Silu)
+        rows_of_powers = keep.tile([P, ROW_TILES // TILES, P], F32)
 
-        b1_cols = keep.tile([P, HID_TILES], F32)
-        b2_all = keep.tile([P, LATENT], F32)
-
-        def widen_biases():
-            nc.vector.tensor_copy(out=b1_cols[:], in_=b1_bf[:])
-            nc.vector.tensor_copy(out=b2_all[:], in_=b2_bf[:])
+        def place_tables():
+            bank = psum_z.tile([P, 2, PAIRS], F32, tag="z")
+            for part in range(2):
+                nc.tensor.transpose(
+                    bank[:, part, :], coef[:, part].rearrange("i a k -> i (a k)"), identity[:]
+                )
+            for a in range(TILES):
+                rows = slice(TERMS * a, TERMS * a + TERMS)
+                nc.scalar.copy(out=blocks[rows, :, a, :], in_=bank[rows, :, :])
+            for half in range(2):
+                bank = psum_z.tile([P, TILES, P], F32, tag="z")
+                for g4 in range(TILES):
+                    g = TILES * half + g4
+                    nc.tensor.transpose(
+                        bank[:, g4, :],
+                        tpow[:, TILES * g : TILES * g + TILES, :].rearrange("r t k -> r (t k)"),
+                        identity[:],
+                    )
+                nc.scalar.copy(
+                    out=rows_of_powers[:, TILES * half : TILES * half + TILES, :], in_=bank[:]
+                )
 
         w1_grouped = keep.tile([P, HID, PACK], BF16, align_bytes=64)
         w1_codes = keep.tile([P, HID], U32, align_bytes=64)
         w1_scales = keep.tile([P, HID], U8, align_bytes=64)
-        w1_halves = [slice(0, HID // 2), slice(HID // 2, HID)]
 
-        def regroup_w1():
-            for cols in w1_halves:
-                regroup(nc.vector.tensor_copy, w1_grouped[:, cols, :], w1_raw[:, :, cols])
+        def regroup_w1(half):
+            regroup(nc.vector.tensor_copy, w1_grouped[:, W1_HALVES[half], :], w1_raw[half][:])
 
-        def quantise_w1():
-            for cols in w1_halves:
-                quantise(nc, w1_codes[:, cols], w1_scales[:, cols], w1_grouped[:, cols, :])
+        def quantise_w1(half):
+            cols = W1_HALVES[half]
+            quantise(nc, w1_codes[:, cols], w1_scales[:, cols], w1_grouped[:, cols, :])
 
         w2_grouped = keep.tile([P, PASSES2, LATENT, PACK], BF16, align_bytes=64)
         w2_codes = keep.tile([P, PASSES2, LATENT], U32, align_bytes=64)
@@ -170,14 +261,18 @@ def tile_koopmanae_pa_t_kernel(
 
         x_banks, x_grouped, x_codes, x_scales = {}, {}, {}, {}
         h_planes, h_grouped, h_codes, h_scales = {}, {}, {}, {}
-        turn_functions, distance, turn_factors = {}, {}, {}
+        turn_factors = {}
         enc_banks, enc, straight, crossed = {}, {}, {}, {}
-        out_pred = out_0.rearrange("(c a r) f -> c r a f", a=TILES, r=P)
-        out_enc = out_1.rearrange("(c a r) f -> c r a f", a=TILES, r=P)
+
+        def halves(c):
+            return range(CHUNK_TILES[c] // 2)
+
+        def out_rows(out, c):
+            return out[rows_of(c), :].rearrange("(a r) f -> r a f", r=P)
 
         def transpose_x(c, half):
             words = x_sb[c][:].bitcast(F32)
-            bank = psum_small.tile([P, 2, 2, P], F32, tag="small")
+            bank = psum_z.tile([P, 2, 2, P], F32, tag="z")
             for a2 in range(2):
                 for u in range(2):
                     nc.tensor.transpose(
@@ -197,71 +292,83 @@ def tile_koopmanae_pa_t_kernel(
         def quantise_x(c):
             x_codes[c] = three.tile([P, CHUNK], U32, name="x_codes", align_bytes=64)
             x_scales[c] = three.tile([P, CHUNK], U8, name="x_scales", align_bytes=64)
-            quantise(nc, x_codes[c][:], x_scales[c][:], x_grouped[c][:])
+            n = P * CHUNK_TILES[c]
+            quantise(nc, x_codes[c][:, 0:n], x_scales[c][:, 0:n], x_grouped[c][:, 0:n, :])
 
         def hidden(c, tiles):
+            n = P * CHUNK_TILES[c]
+            if c not in h_planes:
+                h_planes[c] = three.tile([P, PACK, PASSES2, n], BF16, name="h_planes")
             for m in tiles:
                 units = slice(P * m, P * m + P)
                 z = psum_z.tile([P, CHUNK], F32, tag="z")
                 nc.tensor.matmul_mx(
-                    out=z[:],
+                    out=z[:, 0:n],
                     lhsT=w1_codes[:, units].bitcast(FP8X4),
                     lhsT_scale=w1_scales[:, units],
-                    rhs=x_codes[c][:].bitcast(FP8X4),
-                    rhs_scale=x_scales[c][:],
+                    rhs=x_codes[c][:, 0:n].bitcast(FP8X4),
+                    rhs_scale=x_scales[c][:, 0:n],
                     start=True,
                     stop=True,
                 )
                 nc.scalar.activation(
-                    out=h_planes[c][:, m, :], in_=z[:], func=ACT.Tanh, bias=b1_cols[:, m : m + 1]
+                    out=h_planes[c][:, m % PACK, m // PACK, :],
+                    in_=z[:, 0:n],
+                    func=ACT.Tanh,
+                    bias=columns[:, ROW_B1 + m : ROW_B1 + m + 1],
                 )
 
-        def sine(c):
-            angle4 = psum_small.tile([P, TILES, PAIRS], F32, tag="small")
-            outer_product(angle4, c, freq_all)
-            turn_functions[c] = three.tile([P, 2, TILES, PAIRS], F32, name="turn_functions")
-            nc.scalar.activation(
-                out=turn_functions[c][:, 1], in_=angle4[:], func=ACT.Sin, scale=0.25, bias=-math.pi
-            )
-            distance[c] = two.tile([P, TILES, PAIRS], F32, name="distance")
-            nc.scalar.activation(
-                out=distance[c][:], in_=angle4[:], func=ACT.Abs, scale=0.25, bias=-math.pi
-            )
+        def make_factor(c, part):
+            bank = psum_turn.tile([P, TILES, PAIRS], F32, name="turn_%d" % part)
+            done = 0
+            while done < CHUNK_TILES[c]:
+                g, a = divmod(FIRST_TILE[c] + done, TILES)
+                n = min(TILES - a, CHUNK_TILES[c] - done)
+                nc.tensor.matmul(
+                    out=bank[:, done : done + n, :].rearrange("r a i -> r (a i)"),
+                    lhsT=rows_of_powers[:, g, :],
+                    rhs=blocks[:, part, a : a + n, :].rearrange("k a i -> k (a i)"),
+                    start=True,
+                    stop=True,
+                )
+                done += n
+            turn_factors[c, part] = bank
 
-        def cosine(c):
-            nc.scalar.activation(
-                out=turn_functions[c][:, 0], in_=distance[c][:], func=ACT.Sin, bias=-0.5 * math.pi
-            )
+        def regroup_h(c, copy, first_word, last_word):
+            if c not in h_grouped:
+                h_grouped[c] = two.tile(
+                    [P, PASSES2 * P * CHUNK_TILES[c], PACK], BF16, name="h_grouped", align_bytes=64
+                )
+            words = slice(first_word, last_word)
+            planes = h_planes[c][:].rearrange("p t g r -> p t (g r)")
+            regroup(copy, h_grouped[c][:, words, :], planes[:, :, words])
 
-        def grow(c):
-            n = TILES * PAIRS
-            turn_factors[c] = two.tile([P, 2, n], F32, name="turn_factors")
-            nc.vector.tensor_mul(
-                out=turn_factors[c][:],
-                in0=turn_functions[c][:].rearrange("p s a i -> p s (a i)"),
-                in1=growth[:, c].rearrange("p a i -> p (a i)").unsqueeze(1).to_broadcast([P, 2, n]),
-            )
+        def vector_words(c):
+            return (PASSES2 * CHUNK - SCALAR_WORDS) * CHUNK_TILES[c] // TILES
 
-        def regroup_h(c, g, copy, rows):
-            planes = h_planes[c][:, PACK * g : PACK * g + PACK, rows]
-            regroup(copy, h_grouped[c][:, g, rows, :], planes)
+        def regroup_vector(c):
+            regroup_h(c, nc.vector.tensor_copy, 0, vector_words(c))
+
+        def regroup_scalar(c):
+            regroup_h(c, nc.scalar.copy, vector_words(c), PASSES2 * P * CHUNK_TILES[c])
 
         def quantise_h(c):
-            h_codes[c] = two.tile([P, PASSES2, CHUNK], U32, name="h_codes", align_bytes=64)
-            h_scales[c] = two.tile([P, PASSES2, CHUNK], U8, name="h_scales", align_bytes=64)
-            for g in range(PASSES2):
-                quantise(nc, h_codes[c][:, g], h_scales[c][:, g], h_grouped[c][:, g])
+            words = PASSES2 * P * CHUNK_TILES[c]
+            h_codes[c] = two.tile([P, words], U32, name="h_codes", align_bytes=64)
+            h_scales[c] = two.tile([P, words], U8, name="h_scales", align_bytes=64)
+            quantise(nc, h_codes[c][:], h_scales[c][:], h_grouped[c][:])
 
         def encode(c):
-            for half in range(2):
+            for half in halves(c):
                 bank = psum_enc.tile([P, 2, LATENT], F32, name="enc_bank")
                 for a2 in range(2):
-                    rows = slice(P * (2 * half + a2), P * (2 * half + a2) + P)
                     for g in range(PASSES2):
+                        word = P * (CHUNK_TILES[c] * g + 2 * half + a2)
+                        words = slice(word, word + P)
                         nc.tensor.matmul_mx(
                             out=bank[:, a2, :],
-                            lhsT=h_codes[c][:, g, rows].bitcast(FP8X4),
-                            lhsT_scale=h_scales[c][:, g, rows],
+                            lhsT=h_codes[c][:, words].bitcast(FP8X4),
+                            lhsT_scale=h_scales[c][:, words],
                             rhs=w2_codes[:, g, :].bitcast(FP8X4),
                             rhs_scale=w2_scales[:, g, :],
                             start=(g == 0),
@@ -271,101 +378,123 @@ def tile_koopmanae_pa_t_kernel(
 
         def add_bias2(c):
             enc[c] = three.tile([P, TILES, LATENT], F32, name="enc")
-            for half in range(2):
+            for half in halves(c):
                 nc.vector.tensor_add(
                     out=enc[c][:, 2 * half : 2 * half + 2, :],
                     in0=enc_banks[c, half][:],
                     in1=b2_all[:].unsqueeze(1).to_broadcast([P, 2, LATENT]),
                 )
-            nc.sync.dma_start(out=out_enc[c], in_=enc[c][:])
+            nc.sync.dma_start(out=out_rows(out_1, c), in_=enc[c][:, 0 : CHUNK_TILES[c], :])
 
-        def turn_products(c):
-            n = TILES * PAIRS
-            pairs = enc[c][:].rearrange("p a (i h) -> p (a i) h", h=2)
-            cos_grown, minus_sin_grown = turn_factors[c][:, 0, :], turn_factors[c][:, 1, :]
-            straight[c] = two.tile([P, n, 2], F32, name="straight")
-            for half in (slice(0, n // 2), slice(n // 2, n)):
-                nc.vector.tensor_mul(
-                    out=straight[c][:, half, :],
-                    in0=pairs[:, half, :],
-                    in1=cos_grown[:, half].unsqueeze(2).to_broadcast([P, n // 2, 2]),
-                )
-            crossed[c] = two.tile([P, 2, n], F32, name="crossed")
-            nc.vector.tensor_mul(out=crossed[c][:, 0, :], in0=pairs[:, :, 1], in1=minus_sin_grown)
+        def pairs_of(c):
+            return enc[c][:].rearrange("p a (i h) -> p (a i) h", h=2)
+
+        def turn_straight(c):
+            n = CHUNK_TILES[c] * PAIRS
+            cos_grown = turn_factors[c, 0][:].rearrange("p a i -> p (a i)")[:, 0:n]
+            straight[c] = two.tile([P, TILES * PAIRS, 2], F32, name="straight")
+            nc.vector.tensor_mul(
+                out=straight[c][:, 0:n, :],
+                in0=pairs_of(c)[:, 0:n, :],
+                in1=cos_grown.unsqueeze(2).to_broadcast([P, n, 2]),
+            )
+
+        def turn_crossed(c):
+            n = CHUNK_TILES[c] * PAIRS
+            sin_grown = turn_factors[c, 1][:].rearrange("p a i -> p (a i)")[:, 0:n]
+            crossed[c] = two.tile([P, 2, TILES * PAIRS], F32, name="crossed")
             nc.vector.scalar_tensor_tensor(
-                out=crossed[c][:, 1, :],
-                in0=pairs[:, :, 0],
+                out=crossed[c][:, 0, 0:n],
+                in0=pairs_of(c)[:, 0:n, 1],
                 scalar=-1.0,
-                in1=minus_sin_grown,
+                in1=sin_grown,
                 op0=ALU.mult,
                 op1=ALU.mult,
             )
+            nc.vector.tensor_mul(
+                out=crossed[c][:, 1, 0:n], in0=pairs_of(c)[:, 0:n, 0], in1=sin_grown
+            )
 
         def turn_sum(c):
+            n = CHUNK_TILES[c] * PAIRS
             pred = three.tile([P, TILES * PAIRS, 2], F32)
             nc.vector.tensor_add(
-                out=pred[:], in0=straight[c][:], in1=crossed[c][:].rearrange("p h n -> p n h")
+                out=pred[:, 0:n, :],
+                in0=straight[c][:, 0:n, :],
+                in1=crossed[c][:, :, 0:n].rearrange("p h n -> p n h"),
             )
             nc.sync.dma_start(
-                out=out_pred[c], in_=pred[:].rearrange("p (a i) h -> p a (i h)", a=TILES)
+                out=out_rows(out_0, c),
+                in_=pred[:, 0:n, :].rearrange("p (a i) h -> p a (i h)", i=PAIRS),
             )
 
-        split_ln_amplitudes()
-        transpose_x(0, 0)
-        transpose_x(0, 1)
-        amplitude_powers()
-        choose_table_set()
-        copy_x(0, 0, nc.vector.tensor_copy)
-        copy_x(0, 1, nc.vector.tensor_copy)
-        widen_biases()
-        regroup_w1()
-        quantise_x(0)
-        quantise_w1()
-        transpose_x(1, 0)
-        transpose_x(1, 1)
-        copy_x(1, 0, nc.vector.tensor_copy)
-        copy_x(1, 1, nc.vector.tensor_copy)
-        regroup_w2()
-        quantise_x(1)
-        quantise_w2()
+        def prepare_x(c):
+            for half in halves(c):
+                transpose_x(c, half)
+            for half in halves(c):
+                copy_x(c, half, nc.scalar.copy)
 
-        vector_rows = slice(0, CHUNK - SCALAR_ROWS)
-        scalar_rows = slice(CHUNK - SCALAR_ROWS, CHUNK)
+        inverse_factorials()
+        spread = spread_vectors()
+        powers()
+        coefficients()
+        prepare_x(0)
+        nc.scalar.activation(out=table_choice[:], in_=first[:], func=ACT.Tanh)
+        nc.vector.tensor_copy(out=b2_all[:], in_=spread[:])
+        regroup_w1(0)
+        quantise_x(0)
+        quantise_w1(0)
+        hidden(0, range(0, 4))
+        regroup_w1(1)
+        prepare_x(1)
+        quantise_w1(1)
+        hidden(0, range(4, 8))
+        quantise_x(1)
+        regroup_w2()
 
         def live(c):
             return 0 <= c < N_CHUNKS
 
         for c in range(N_CHUNKS + 1):
             if live(c):
-                h_planes[c] = three.tile([P, HID_TILES, CHUNK], BF16, name="h_planes")
-                hidden(c, range(0, Z_BANKS))
+                hidden(c, range(2, 6) if c > 0 else range(0))
             if live(c - 1):
                 encode(c - 1)
-                add_bias2(c - 1)
-                turn_products(c - 1)
             if live(c):
-                hidden(c, range(Z_BANKS, HID_TILES))
-                h_grouped[c] = two.tile(
-                    [P, PASSES2, CHUNK, PACK], BF16, name="h_grouped", align_bytes=64
-                )
-                regroup_h(c, 0, nc.vector.tensor_copy, vector_rows)
+                hidden(c, range(6, 8) if c > 0 else range(0))
+            if c == 1:
+                place_tables()
+            if c == 2:
+                turn_straight(0)
+                turn_crossed(0)
+                make_factor(1, 0)
+                make_factor(1, 1)
             if live(c - 1):
-                turn_sum(c - 1)
+                add_bias2(c - 1)
             if live(c):
-                regroup_h(c, 1, nc.vector.tensor_copy, vector_rows)
-                sine(c)
+                regroup_vector(c)
+                regroup_scalar(c)
+            if c >= 2:
+                turn_straight(c - 1)
+                turn_crossed(c - 1)
             if live(c + 2):
-                transpose_x(c + 2, 0)
-            if live(c):
-                regroup_h(c, 0, nc.scalar.copy, scalar_rows)
-                regroup_h(c, 1, nc.scalar.copy, scalar_rows)
-                cosine(c)
-            if live(c + 2):
-                transpose_x(c + 2, 1)
-                copy_x(c + 2, 0, nc.scalar.copy)
-                copy_x(c + 2, 1, nc.scalar.copy)
+                prepare_x(c + 2)
+            if c == 0:
+                quantise_w2()
+            if 2 <= c < N_CHUNKS:
+                make_factor(c, 0)
+            if live(c + 1):
+                hidden(c + 1, range(0, 2))
+            if c == 1:
+                make_factor(0, 0)
+                make_factor(0, 1)
+            if 2 <= c < N_CHUNKS:
+                make_factor(c, 1)
             if live(c):
                 quantise_h(c)
-                grow(c)
+            if c == 2:
+                turn_sum(0)
+            if c >= 2:
+                turn_sum(c - 1)
             if live(c + 2):
                 quantise_x(c + 2)

@@ -26,7 +26,7 @@ HID_TILES = HID // P
 PASSES2 = HID // (P * PACK)
 TERMS = 32
 ROW_AMP, ROW_FREQ, ROW_B1, ROW_B2, VEC_ROWS = 32, 33, 34, 42, 44
-SCALAR_WORDS = 384
+SCALAR_SHARE = [0, 0, 0, 384, 384, 384, 384, 512, 1024]
 Z_BANKS = 4
 
 FLOPS = 2 * ROWS * D_IN * HID + 2 * ROWS * HID * LATENT
@@ -63,15 +63,17 @@ def tile_koopmanae_pa_t_kernel(
 
         vec = keep.tile([P, P], BF16)
         nc.vector.memset(vec[:].bitcast(I32), 0)
-        nc.sync.dma_start(out=vec[0:ROW_AMP, :], in_=delta_t.rearrange("(t r) -> t r", r=P))
-        nc.sync.dma_start(
-            out=vec[ROW_AMP:ROW_FREQ, :], in_=amplitudes.rearrange("(o i) -> o i", o=1)
-        )
-        nc.sync.dma_start(
-            out=vec[ROW_FREQ:ROW_B1, :], in_=frequencies.rearrange("(o i) -> o i", o=1)
-        )
-        nc.sync.dma_start(out=vec[ROW_B1:ROW_B2, :], in_=b_enc1.rearrange("(m p) -> m p", p=P))
-        nc.sync.dma_start(out=vec[ROW_B2:VEC_ROWS, :], in_=b_enc2.rearrange("(m p) -> m p", p=P))
+
+        def load_vectors():
+            nc.sync.dma_start(out=vec[0:ROW_AMP, :], in_=delta_t.rearrange("(t r) -> t r", r=P))
+            nc.sync.dma_start(
+                out=vec[ROW_AMP:ROW_FREQ, :], in_=amplitudes.rearrange("(o i) -> o i", o=1)
+            )
+            nc.sync.dma_start(
+                out=vec[ROW_FREQ:ROW_B1, :], in_=frequencies.rearrange("(o i) -> o i", o=1)
+            )
+            nc.sync.dma_start(out=vec[ROW_B1:ROW_B2, :], in_=b_enc1.rearrange("(m p) -> m p", p=P))
+            nc.sync.dma_start(out=vec[ROW_B2:VEC_ROWS, :], in_=b_enc2.rearrange("(m p) -> m p", p=P))
 
         def rows_of(c):
             return slice(P * FIRST_TILE[c], P * (FIRST_TILE[c] + CHUNK_TILES[c]))
@@ -94,12 +96,22 @@ def tile_koopmanae_pa_t_kernel(
             for u in range(2):
                 nc.sync.dma_start(out=raw[:, 2 * u : 2 * u + 2, :], in_=w1_rows[:, u, :, cols])
             w1_raw.append(raw)
+            if half == 0:
+                load_vectors()
         load_x(1)
         w2_raw = keep.tile([P, HID_TILES, LATENT], BF16)
         nc.sync.dma_start(out=w2_raw[:], in_=W_enc2.rearrange("(m p) f -> p m f", p=P))
         for c in range(2, N_CHUNKS):
             load_x(c)
 
+        counts = keep.tile([P, TERMS - 1], F32)
+        nc.gpsimd.iota(
+            counts[:],
+            pattern=[[1, TERMS - 1]],
+            base=1,
+            channel_multiplier=0,
+            allow_small_or_imprecise_dtypes=True,
+        )
         identity = keep.tile([P, P], F32)
         make_identity(nc, identity[:])
         identity_bf = keep.tile([P, P], BF16)
@@ -118,14 +130,6 @@ def tile_koopmanae_pa_t_kernel(
         nc.gpsimd.memset(zpow[:, 1, 0:1], 0.0)
         tpow = keep.tile([P, ROW_TILES, TERMS], F32)
         nc.gpsimd.memset(tpow[:, :, 0:1], 1.0)
-        counts = keep.tile([P, TERMS - 1], F32)
-        nc.gpsimd.iota(
-            counts[:],
-            pattern=[[1, TERMS - 1]],
-            base=1,
-            channel_multiplier=0,
-            allow_small_or_imprecise_dtypes=True,
-        )
         inverses = keep.tile([P, TERMS - 1], F32)
         zeros = keep.tile([P, TERMS - 1], F32)
         inv_fact = keep.tile([P, TERMS], F32)
@@ -209,34 +213,37 @@ def tile_koopmanae_pa_t_kernel(
 
         rows_of_powers = keep.tile([P, ROW_TILES // TILES, P], F32)
 
-        def place_tables():
-            bank = psum_z.tile([P, 2, PAIRS], F32, tag="z")
+        def place_coefficients():
+            bank = psum_turn.tile([P, 2, PAIRS], F32, tag="turn_0")
             for part in range(2):
                 nc.tensor.transpose(
                     bank[:, part, :], coef[:, part].rearrange("i a k -> i (a k)"), identity[:]
                 )
             for a in range(TILES):
                 rows = slice(TERMS * a, TERMS * a + TERMS)
-                nc.scalar.copy(out=blocks[rows, :, a, :], in_=bank[rows, :, :])
-            for half in range(2):
-                bank = psum_z.tile([P, TILES, P], F32, tag="z")
-                for g4 in range(TILES):
-                    g = TILES * half + g4
-                    nc.tensor.transpose(
-                        bank[:, g4, :],
-                        tpow[:, TILES * g : TILES * g + TILES, :].rearrange("r t k -> r (t k)"),
-                        identity[:],
-                    )
-                nc.scalar.copy(
-                    out=rows_of_powers[:, TILES * half : TILES * half + TILES, :], in_=bank[:]
+                nc.vector.tensor_copy(out=blocks[rows, :, a, :], in_=bank[rows, :, :])
+
+        def place_powers(half):
+            bank = psum_turn.tile([P, TILES, P], F32, tag="turn_%d" % half)
+            for g4 in range(TILES):
+                g = TILES * half + g4
+                nc.tensor.transpose(
+                    bank[:, g4, :],
+                    tpow[:, TILES * g : TILES * g + TILES, :].rearrange("r t k -> r (t k)"),
+                    identity[:],
                 )
+            nc.vector.tensor_copy(
+                out=rows_of_powers[:, TILES * half : TILES * half + TILES, :], in_=bank[:]
+            )
 
         w1_grouped = keep.tile([P, HID, PACK], BF16, align_bytes=64)
         w1_codes = keep.tile([P, HID], U32, align_bytes=64)
         w1_scales = keep.tile([P, HID], U8, align_bytes=64)
 
-        def regroup_w1(half):
-            regroup(nc.vector.tensor_copy, w1_grouped[:, W1_HALVES[half], :], w1_raw[half][:])
+        def regroup_w1(half, copy, first_col, last_col):
+            grouped = w1_grouped[:, W1_HALVES[half], :]
+            cols = slice(first_col, last_col)
+            regroup(copy, grouped[:, cols, :], w1_raw[half][:, :, cols])
 
         def quantise_w1(half):
             cols = W1_HALVES[half]
@@ -246,10 +253,10 @@ def tile_koopmanae_pa_t_kernel(
         w2_codes = keep.tile([P, PASSES2, LATENT], U32, align_bytes=64)
         w2_scales = keep.tile([P, PASSES2, LATENT], U8, align_bytes=64)
 
-        def regroup_w2():
+        def regroup_w2(copy):
             for g in range(PASSES2):
                 planes = w2_raw[:, PACK * g : PACK * g + PACK, :]
-                regroup(nc.vector.tensor_copy, w2_grouped[:, g], planes)
+                regroup(copy, w2_grouped[:, g], planes)
 
         def quantise_w2():
             quantise(
@@ -270,9 +277,19 @@ def tile_koopmanae_pa_t_kernel(
         def out_rows(out, c):
             return out[rows_of(c), :].rearrange("(a r) f -> r a f", r=P)
 
+        bank_of = {
+            (1, 0): (psum_enc, "enc_bank"),
+            (1, 1): (psum_enc, "enc_bank"),
+            (2, 0): (psum_turn, "turn_0"),
+            (2, 1): (psum_turn, "turn_1"),
+            (3, 0): (psum_enc, "enc_bank"),
+            (3, 1): (psum_enc, "enc_bank"),
+        }
+
         def transpose_x(c, half):
             words = x_sb[c][:].bitcast(F32)
-            bank = psum_z.tile([P, 2, 2, P], F32, tag="z")
+            pool, tag = bank_of.get((c, half), (psum_z, "z"))
+            bank = pool.tile([P, 2, 2, P], F32, tag=tag)
             for a2 in range(2):
                 for u in range(2):
                     nc.tensor.transpose(
@@ -319,7 +336,7 @@ def tile_koopmanae_pa_t_kernel(
                 )
 
         def make_factor(c, part):
-            bank = psum_turn.tile([P, TILES, PAIRS], F32, name="turn_%d" % part)
+            bank = psum_turn.tile([P, TILES, PAIRS], F32, tag="turn_%d" % part)
             done = 0
             while done < CHUNK_TILES[c]:
                 g, a = divmod(FIRST_TILE[c] + done, TILES)
@@ -339,12 +356,14 @@ def tile_koopmanae_pa_t_kernel(
                 h_grouped[c] = two.tile(
                     [P, PASSES2 * P * CHUNK_TILES[c], PACK], BF16, name="h_grouped", align_bytes=64
                 )
+            if first_word == last_word:
+                return
             words = slice(first_word, last_word)
             planes = h_planes[c][:].rearrange("p t g r -> p t (g r)")
             regroup(copy, h_grouped[c][:, words, :], planes[:, :, words])
 
         def vector_words(c):
-            return (PASSES2 * CHUNK - SCALAR_WORDS) * CHUNK_TILES[c] // TILES
+            return (PASSES2 * CHUNK - SCALAR_SHARE[c]) * CHUNK_TILES[c] // TILES
 
         def regroup_vector(c):
             regroup_h(c, nc.vector.tensor_copy, 0, vector_words(c))
@@ -360,7 +379,7 @@ def tile_koopmanae_pa_t_kernel(
 
         def encode(c):
             for half in halves(c):
-                bank = psum_enc.tile([P, 2, LATENT], F32, name="enc_bank")
+                bank = psum_enc.tile([P, 2, LATENT], F32, tag="enc_bank")
                 for a2 in range(2):
                     for g in range(PASSES2):
                         word = P * (CHUNK_TILES[c] * g + 2 * half + a2)
@@ -392,7 +411,7 @@ def tile_koopmanae_pa_t_kernel(
         def turn_straight(c):
             n = CHUNK_TILES[c] * PAIRS
             cos_grown = turn_factors[c, 0][:].rearrange("p a i -> p (a i)")[:, 0:n]
-            straight[c] = two.tile([P, TILES * PAIRS, 2], F32, name="straight")
+            straight[c] = three.tile([P, TILES * PAIRS, 2], F32, name="straight")
             nc.vector.tensor_mul(
                 out=straight[c][:, 0:n, :],
                 in0=pairs_of(c)[:, 0:n, :],
@@ -402,7 +421,7 @@ def tile_koopmanae_pa_t_kernel(
         def turn_crossed(c):
             n = CHUNK_TILES[c] * PAIRS
             sin_grown = turn_factors[c, 1][:].rearrange("p a i -> p (a i)")[:, 0:n]
-            crossed[c] = two.tile([P, 2, TILES * PAIRS], F32, name="crossed")
+            crossed[c] = three.tile([P, 2, TILES * PAIRS], F32, name="crossed")
             nc.vector.scalar_tensor_tensor(
                 out=crossed[c][:, 0, 0:n],
                 in0=pairs_of(c)[:, 0:n, 1],
@@ -415,10 +434,12 @@ def tile_koopmanae_pa_t_kernel(
                 out=crossed[c][:, 1, 0:n], in0=pairs_of(c)[:, 0:n, 0], in1=sin_grown
             )
 
-        def turn_sum(c):
+        waited_for = keep.tile([P, 1], U32)
+
+        def turn_sum(c, engine):
             n = CHUNK_TILES[c] * PAIRS
             pred = three.tile([P, TILES * PAIRS, 2], F32)
-            nc.vector.tensor_add(
+            engine.tensor_add(
                 out=pred[:, 0:n, :],
                 in0=straight[c][:, 0:n, :],
                 in1=crossed[c][:, :, 0:n].rearrange("p h n -> p n h"),
@@ -428,73 +449,82 @@ def tile_koopmanae_pa_t_kernel(
                 in_=pred[:, 0:n, :].rearrange("p (a i) h -> p a (i h)", i=PAIRS),
             )
 
-        def prepare_x(c):
+        def hold_sum(c):
+            nc.gpsimd.tensor_copy(out=waited_for[:], in_=h_codes[c][:, 0:1])
+
+        def prepare_x(c, copy):
             for half in halves(c):
                 transpose_x(c, half)
             for half in halves(c):
-                copy_x(c, half, nc.scalar.copy)
+                copy_x(c, half, copy)
 
         inverse_factorials()
+        prepare_x(0, nc.vector.tensor_copy)
         spread = spread_vectors()
+        regroup_w1(0, nc.vector.tensor_copy, 0, 320)
+        regroup_w1(0, nc.scalar.copy, 320, 512)
         powers()
         coefficients()
-        prepare_x(0)
         nc.scalar.activation(out=table_choice[:], in_=first[:], func=ACT.Tanh)
-        nc.vector.tensor_copy(out=b2_all[:], in_=spread[:])
-        regroup_w1(0)
         quantise_x(0)
         quantise_w1(0)
         hidden(0, range(0, 4))
-        regroup_w1(1)
-        prepare_x(1)
+        regroup_w1(1, nc.vector.tensor_copy, 0, 512)
+        nc.vector.tensor_copy(out=b2_all[:], in_=spread[:])
         quantise_w1(1)
+        prepare_x(1, nc.vector.tensor_copy)
         hidden(0, range(4, 8))
         quantise_x(1)
-        regroup_w2()
+        prepare_x(2, nc.vector.tensor_copy)
+        hidden(1, range(0, 4))
+        quantise_x(2)
+        regroup_w2(nc.vector.tensor_copy)
+        prepare_x(3, nc.vector.tensor_copy)
+        hidden(1, range(4, 8))
+        place_powers(0)
+        place_powers(1)
+        quantise_w2()
+        hidden(2, range(0, 4))
+        quantise_x(3)
+        regroup_vector(0)
 
         def live(c):
             return 0 <= c < N_CHUNKS
 
-        for c in range(N_CHUNKS + 1):
-            if live(c):
-                hidden(c, range(2, 6) if c > 0 else range(0))
-            if live(c - 1):
-                encode(c - 1)
-            if live(c):
-                hidden(c, range(6, 8) if c > 0 else range(0))
-            if c == 1:
-                place_tables()
-            if c == 2:
-                turn_straight(0)
-                turn_crossed(0)
-                make_factor(1, 0)
-                make_factor(1, 1)
-            if live(c - 1):
-                add_bias2(c - 1)
-            if live(c):
-                regroup_vector(c)
-                regroup_scalar(c)
-            if c >= 2:
-                turn_straight(c - 1)
-                turn_crossed(c - 1)
+        for c in range(2, N_CHUNKS + 3):
+            if c > 3 and live(c - 3):
+                make_factor(c - 3, 0)
             if live(c + 2):
-                prepare_x(c + 2)
-            if c == 0:
-                quantise_w2()
-            if 2 <= c < N_CHUNKS:
-                make_factor(c, 0)
-            if live(c + 1):
-                hidden(c + 1, range(0, 2))
-            if c == 1:
+                prepare_x(c + 2, nc.scalar.copy)
+            if c > 3 and live(c - 3):
+                make_factor(c - 3, 1)
+            if live(c):
+                hidden(c, range(4, 8))
+            if c == 3:
                 make_factor(0, 0)
                 make_factor(0, 1)
-            if 2 <= c < N_CHUNKS:
-                make_factor(c, 1)
+            if c > 3 and live(c - 2):
+                regroup_vector(c - 2)
+            if live(c - 3):
+                add_bias2(c - 3)
+            if live(c - 2):
+                quantise_h(c - 2)
             if live(c):
-                quantise_h(c)
-            if c == 2:
-                turn_sum(0)
-            if c >= 2:
-                turn_sum(c - 1)
+                regroup_scalar(c)
+            if live(c - 2):
+                encode(c - 2)
+            if live(c + 1):
+                hidden(c + 1, range(0, 4))
+            if live(c - 3):
+                turn_straight(c - 3)
+                turn_crossed(c - 3)
+            if live(c - 4):
+                if live(c - 2):
+                    hold_sum(c - 2)
+                turn_sum(c - 4, nc.gpsimd)
             if live(c + 2):
                 quantise_x(c + 2)
+            if c == 2:
+                regroup_vector(1)
+                place_coefficients()
+        turn_sum(N_CHUNKS - 1, nc.vector)

@@ -171,25 +171,24 @@ def tile_koopmanae_pa_t_kernel(
                 out=zpow[:, 0, 1:2], in_=columns[:, ROW_AMP:ROW_FREQ], func=ACT.Ln
             )
             nc.gpsimd.tensor_copy(out=zpow[:, 1, 1:2], in_=columns[:, ROW_FREQ:ROW_B1])
-            by_re = keep.tile([P, 2, TERMS // 2], F32)
-            by_im = keep.tile([P, 2, TERMS // 2], F32)
+            products = keep.tile([P, 2, 2, TERMS // 2], F32)
             m = 1
             while m < TERMS - 1:
                 n = min(m, TERMS - 1 - m)
-                for part, scaled in ((0, by_re), (1, by_im)):
-                    nc.gpsimd.tensor_scalar(
-                        out=scaled[:, :, 0:n],
-                        in0=zpow[:, :, 1 : 1 + n],
-                        scalar1=zpow[:, part, m : m + 1],
-                        scalar2=0.0,
-                        op0=ALU.mult,
-                        op1=ALU.add,
-                    )
+                nc.gpsimd.tensor_mul(
+                    out=products[:, :, :, 0:n],
+                    in0=zpow[:, :, 1 : 1 + n].unsqueeze(1).to_broadcast([P, 2, 2, n]),
+                    in1=zpow[:, :, m : m + 1].unsqueeze(3).to_broadcast([P, 2, 2, n]),
+                )
                 nc.gpsimd.tensor_sub(
-                    out=zpow[:, 0, m + 1 : m + 1 + n], in0=by_re[:, 0, 0:n], in1=by_im[:, 1, 0:n]
+                    out=zpow[:, 0, m + 1 : m + 1 + n],
+                    in0=products[:, 0, 0, 0:n],
+                    in1=products[:, 1, 1, 0:n],
                 )
                 nc.gpsimd.tensor_add(
-                    out=zpow[:, 1, m + 1 : m + 1 + n], in0=by_re[:, 1, 0:n], in1=by_im[:, 0, 0:n]
+                    out=zpow[:, 1, m + 1 : m + 1 + n],
+                    in0=products[:, 0, 1, 0:n],
+                    in1=products[:, 1, 0, 0:n],
                 )
                 m = 2 * m
             for part in range(2):
@@ -505,8 +504,8 @@ def tile_koopmanae_pa_t_kernel(
                 make_factor(0, 1)
             if c > 3 and live(c - 2):
                 regroup_vector(c - 2)
-            if live(c - 3):
-                add_bias2(c - 3)
+            if c > 2 and live(c + 1):
+                quantise_x(c + 1)
             if live(c - 2):
                 quantise_h(c - 2)
             if live(c):
@@ -515,16 +514,16 @@ def tile_koopmanae_pa_t_kernel(
                 encode(c - 2)
             if live(c + 1):
                 hidden(c + 1, range(0, 4))
+            if c == 2:
+                regroup_vector(1)
+                place_coefficients()
             if live(c - 3):
                 turn_straight(c - 3)
                 turn_crossed(c - 3)
+            if live(c - 2):
+                add_bias2(c - 2)
             if live(c - 4):
                 if live(c - 2):
                     hold_sum(c - 2)
                 turn_sum(c - 4, nc.gpsimd)
-            if live(c + 2):
-                quantise_x(c + 2)
-            if c == 2:
-                regroup_vector(1)
-                place_coefficients()
         turn_sum(N_CHUNKS - 1, nc.vector)

@@ -34,8 +34,8 @@ FLOPS = 2 * ROWS * D_IN * HID + 2 * ROWS * HID * LATENT
 
 def regroup(copy, grouped, planes):
     copy(
-        out=grouped.rearrange("p (c i) t -> p c t i", i=4),
-        in_=planes.rearrange("p t (c i) -> p c t i", i=4),
+        out=grouped.rearrange("p (c i) t -> p c t i", i=8),
+        in_=planes.rearrange("p t (c i) -> p c t i", i=8),
     )
 
 

@@ -126,8 +126,8 @@ def tile_koopmanae_pa_t_kernel(
         blocks = keep.tile([P, 2, TILES, PAIRS], F32)
         nc.gpsimd.memset(blocks[:], 0.0)
         zpow = keep.tile([P, 2, TERMS], F32)
-        nc.gpsimd.memset(zpow[:, 0, 0:1], 1.0)
-        nc.gpsimd.memset(zpow[:, 1, 0:1], 0.0)
+        nc.vector.memset(zpow[:, 0, 0:1], 1.0)
+        nc.vector.memset(zpow[:, 1, 0:1], 0.0)
         tpow = keep.tile([P, ROW_TILES, TERMS], F32)
         nc.gpsimd.memset(tpow[:, :, 0:1], 1.0)
         inverses = keep.tile([P, TERMS - 1], F32)
@@ -166,33 +166,42 @@ def tile_koopmanae_pa_t_kernel(
                 )
             return spread
 
-        def coefficients():
+        def first_power():
             nc.scalar.activation(
                 out=zpow[:, 0, 1:2], in_=columns[:, ROW_AMP:ROW_FREQ], func=ACT.Ln
             )
-            nc.gpsimd.tensor_copy(out=zpow[:, 1, 1:2], in_=columns[:, ROW_FREQ:ROW_B1])
-            products = keep.tile([P, 2, 2, TERMS // 2], F32)
-            m = 1
-            while m < TERMS - 1:
-                n = min(m, TERMS - 1 - m)
-                nc.gpsimd.tensor_mul(
-                    out=products[:, :, :, 0:n],
-                    in0=zpow[:, :, 1 : 1 + n].unsqueeze(1).to_broadcast([P, 2, 2, n]),
-                    in1=zpow[:, :, m : m + 1].unsqueeze(3).to_broadcast([P, 2, 2, n]),
+            nc.vector.tensor_copy(out=zpow[:, 1, 1:2], in_=columns[:, ROW_FREQ:ROW_B1])
+
+        by_im = keep.tile([P, 2, TERMS // 2], F32)
+
+        def power_count(m):
+            return min(m, TERMS - 1 - m)
+
+        def times_imaginary(m):
+            n = power_count(m)
+            nc.vector.tensor_scalar(
+                out=by_im[:, :, 0:n],
+                in0=zpow[:, :, 1 : 1 + n],
+                scalar1=zpow[:, 1, m : m + 1],
+                scalar2=None,
+                op0=ALU.mult,
+            )
+
+        def next_powers(m):
+            n = power_count(m)
+            for part, other, op in ((0, 1, ALU.subtract), (1, 0, ALU.add)):
+                nc.vector.scalar_tensor_tensor(
+                    out=zpow[:, part, m + 1 : m + 1 + n],
+                    in0=zpow[:, part, 1 : 1 + n],
+                    scalar=zpow[:, 0, m : m + 1],
+                    in1=by_im[:, other, 0:n],
+                    op0=ALU.mult,
+                    op1=op,
                 )
-                nc.gpsimd.tensor_sub(
-                    out=zpow[:, 0, m + 1 : m + 1 + n],
-                    in0=products[:, 0, 0, 0:n],
-                    in1=products[:, 1, 1, 0:n],
-                )
-                nc.gpsimd.tensor_add(
-                    out=zpow[:, 1, m + 1 : m + 1 + n],
-                    in0=products[:, 0, 1, 0:n],
-                    in1=products[:, 1, 0, 0:n],
-                )
-                m = 2 * m
+
+        def coefficients():
             for part in range(2):
-                nc.gpsimd.tensor_mul(
+                nc.vector.tensor_mul(
                     out=coef[:, part],
                     in0=zpow[:, part, :].unsqueeze(1).to_broadcast([P, 4, TERMS]),
                     in1=inv_fact[:].unsqueeze(1).to_broadcast([P, 4, TERMS]),
@@ -463,45 +472,53 @@ def tile_koopmanae_pa_t_kernel(
         regroup_w1(0, nc.vector.tensor_copy, 0, 320)
         regroup_w1(0, nc.scalar.copy, 320, 512)
         powers()
-        coefficients()
+        first_power()
         nc.scalar.activation(out=table_choice[:], in_=first[:], func=ACT.Tanh)
         quantise_x(0)
         quantise_w1(0)
         hidden(0, range(0, 4))
         regroup_w1(1, nc.vector.tensor_copy, 0, 512)
+        times_imaginary(1)
         nc.vector.tensor_copy(out=b2_all[:], in_=spread[:])
         quantise_w1(1)
+        next_powers(1)
         prepare_x(1, nc.vector.tensor_copy)
+        times_imaginary(2)
         hidden(0, range(4, 8))
         quantise_x(1)
+        next_powers(2)
         prepare_x(2, nc.vector.tensor_copy)
         hidden(1, range(0, 4))
+        times_imaginary(4)
         quantise_x(2)
+        next_powers(4)
         regroup_w2(nc.vector.tensor_copy)
+        times_imaginary(8)
         prepare_x(3, nc.vector.tensor_copy)
         hidden(1, range(4, 8))
+        next_powers(8)
         place_powers(0)
         place_powers(1)
+        times_imaginary(16)
         quantise_w2()
+        next_powers(16)
         hidden(2, range(0, 4))
         quantise_x(3)
+        coefficients()
         regroup_vector(0)
 
         def live(c):
             return 0 <= c < N_CHUNKS
 
         for c in range(2, N_CHUNKS + 3):
-            if c > 3 and live(c - 3):
+            if live(c - 3):
                 make_factor(c - 3, 0)
             if live(c + 2):
                 prepare_x(c + 2, nc.scalar.copy)
-            if c > 3 and live(c - 3):
+            if live(c - 3):
                 make_factor(c - 3, 1)
             if live(c):
                 hidden(c, range(4, 8))
-            if c == 3:
-                make_factor(0, 0)
-                make_factor(0, 1)
             if c > 3 and live(c - 2):
                 regroup_vector(c - 2)
             if c > 2 and live(c + 1):
@@ -512,11 +529,11 @@ def tile_koopmanae_pa_t_kernel(
                 regroup_scalar(c)
             if live(c - 2):
                 encode(c - 2)
-            if live(c + 1):
-                hidden(c + 1, range(0, 4))
             if c == 2:
                 regroup_vector(1)
                 place_coefficients()
+            if live(c + 1):
+                hidden(c + 1, range(0, 4))
             if live(c - 3):
                 turn_straight(c - 3)
                 turn_crossed(c - 3)

@@ -16,6 +16,7 @@ P = 128
 PACK = 4
 ROWS, D_IN, HID, PAIRS = 4096, 512, 1024, 128
 LATENT = 2 * PAIRS
+BLOCK = 4
 CHUNK = 512
 TILES = CHUNK // P
 ROW_TILES = ROWS // P
@@ -428,18 +429,20 @@ def tile_koopmanae_pa_t_kernel(
 
         def turn_crossed(c):
             n = CHUNK_TILES[c] * PAIRS
+            pairs = pairs_of(c)[:, 0:n, :].rearrange("p (b i) h -> p b i h", i=BLOCK)
             sin_grown = turn_factors[c, 1][:].rearrange("p a i -> p (a i)")[:, 0:n]
-            crossed[c] = three.tile([P, 2, TILES * PAIRS], F32, name="crossed")
+            sin_grown = sin_grown.rearrange("p (b i) -> p b i", i=BLOCK)
+            crossed[c] = three.tile([P, TILES * PAIRS // BLOCK, 2, BLOCK], F32, name="crossed")
             nc.vector.scalar_tensor_tensor(
-                out=crossed[c][:, 0, 0:n],
-                in0=pairs_of(c)[:, 0:n, 1],
+                out=crossed[c][:, 0 : n // BLOCK, 0, :],
+                in0=pairs[:, :, :, 1],
                 scalar=-1.0,
                 in1=sin_grown,
                 op0=ALU.mult,
                 op1=ALU.mult,
             )
             nc.vector.tensor_mul(
-                out=crossed[c][:, 1, 0:n], in0=pairs_of(c)[:, 0:n, 0], in1=sin_grown
+                out=crossed[c][:, 0 : n // BLOCK, 1, :], in0=pairs[:, :, :, 0], in1=sin_grown
             )
 
         waited_for = keep.tile([P, 1], U32)
@@ -448,9 +451,9 @@ def tile_koopmanae_pa_t_kernel(
             n = CHUNK_TILES[c] * PAIRS
             pred = three.tile([P, TILES * PAIRS, 2], F32)
             engine.tensor_add(
-                out=pred[:, 0:n, :],
-                in0=straight[c][:, 0:n, :],
-                in1=crossed[c][:, :, 0:n].rearrange("p h n -> p n h"),
+                out=pred[:, 0:n, :].rearrange("p (b i) h -> p b h i", i=BLOCK),
+                in0=straight[c][:, 0:n, :].rearrange("p (b i) h -> p b h i", i=BLOCK),
+                in1=crossed[c][:, 0 : n // BLOCK],
             )
             nc.sync.dma_start(
                 out=out_rows(out_0, c),

@@ -20,14 +20,14 @@ BLOCK = 4
 CHUNK = 512
 TILES = CHUNK // P
 ROW_TILES = ROWS // P
-CHUNK_TILES = [TILES // 2] + [TILES] * (ROW_TILES // TILES - 1) + [TILES // 2]
+CHUNK_TILES = [2, 4, 4, 4, 4, 4, 4, 2, 2, 2]
 N_CHUNKS = len(CHUNK_TILES)
 FIRST_TILE = [sum(CHUNK_TILES[:c]) for c in range(N_CHUNKS)]
 HID_TILES = HID // P
 PASSES2 = HID // (P * PACK)
 TERMS = 32
 ROW_AMP, ROW_FREQ, ROW_B1, ROW_B2, VEC_ROWS = 32, 33, 34, 42, 44
-SCALAR_SHARE = [0, 0, 0, 384, 384, 384, 384, 512, 1024]
+SCALAR_SHARE = [0, 0, 0, 256, 256, 256, 320, 768, 768, 1024]
 Z_BANKS = 4
 
 FLOPS = 2 * ROWS * D_IN * HID + 2 * ROWS * HID * LATENT
@@ -57,6 +57,7 @@ def tile_koopmanae_pa_t_kernel(
         x_pool = ctx.enter_context(tc.tile_pool(name="x_pool", bufs=N_CHUNKS))
         two = ctx.enter_context(tc.tile_pool(name="two", bufs=2))
         three = ctx.enter_context(tc.tile_pool(name="three", bufs=3))
+        four = ctx.enter_context(tc.tile_pool(name="four", bufs=4))
         psum_z = ctx.enter_context(tc.psum_pool(name="psum_z", bufs=Z_BANKS))
         psum_enc = ctx.enter_context(tc.psum_pool(name="psum_enc", bufs=2))
         psum_turn = ctx.enter_context(tc.psum_pool(name="psum_turn", bufs=1))
@@ -449,7 +450,7 @@ def tile_koopmanae_pa_t_kernel(
 
         def turn_sum(c, engine):
             n = CHUNK_TILES[c] * PAIRS
-            pred = three.tile([P, TILES * PAIRS, 2], F32)
+            pred = four.tile([P, TILES * PAIRS, 2], F32)
             engine.tensor_add(
                 out=pred[:, 0:n, :].rearrange("p (b i) h -> p b h i", i=BLOCK),
                 in0=straight[c][:, 0:n, :].rearrange("p (b i) h -> p b h i", i=BLOCK),
@@ -542,8 +543,9 @@ def tile_koopmanae_pa_t_kernel(
                 turn_crossed(c - 3)
             if live(c - 2):
                 add_bias2(c - 2)
-            if live(c - 4):
+            if live(c - 4) and c - 4 < N_CHUNKS - 2:
                 if live(c - 2):
                     hold_sum(c - 2)
                 turn_sum(c - 4, nc.gpsimd)
-        turn_sum(N_CHUNKS - 1, nc.vector)
+            if N_CHUNKS - 2 <= c - 3 < N_CHUNKS:
+                turn_sum(c - 3, nc.vector)

@@ -27,7 +27,7 @@ HID_TILES = HID // P
 PASSES2 = HID // (P * PACK)
 TERMS = 32
 ROW_AMP, ROW_FREQ, ROW_B1, ROW_B2, VEC_ROWS = 32, 33, 34, 42, 44
-SCALAR_SHARE = [0, 0, 0, 256, 256, 256, 320, 768, 768, 1024]
+SCALAR_SHARE = [64 * c for c in range(7)] + [1024] * 3
 Z_BANKS = 4
 
 FLOPS = 2 * ROWS * D_IN * HID + 2 * ROWS * HID * LATENT
@@ -480,8 +480,9 @@ def tile_koopmanae_pa_t_kernel(
         nc.scalar.activation(out=table_choice[:], in_=first[:], func=ACT.Tanh)
         quantise_x(0)
         quantise_w1(0)
+        regroup_w1(1, nc.scalar.copy, 320, 512)
         hidden(0, range(0, 4))
-        regroup_w1(1, nc.vector.tensor_copy, 0, 512)
+        regroup_w1(1, nc.vector.tensor_copy, 0, 320)
         times_imaginary(1)
         nc.vector.tensor_copy(out=b2_all[:], in_=spread[:])
         quantise_w1(1)
@@ -489,6 +490,7 @@ def tile_koopmanae_pa_t_kernel(
         prepare_x(1, nc.vector.tensor_copy)
         times_imaginary(2)
         hidden(0, range(4, 8))
+        regroup_scalar(0)
         quantise_x(1)
         next_powers(2)
         prepare_x(2, nc.vector.tensor_copy)
@@ -500,6 +502,7 @@ def tile_koopmanae_pa_t_kernel(
         times_imaginary(8)
         prepare_x(3, nc.vector.tensor_copy)
         hidden(1, range(4, 8))
+        regroup_scalar(1)
         next_powers(8)
         place_powers(0)
         place_powers(1)
@@ -521,6 +524,8 @@ def tile_koopmanae_pa_t_kernel(
                 prepare_x(c + 2, nc.scalar.copy)
             if live(c - 3):
                 make_factor(c - 3, 1)
+            if c == 2:
+                place_coefficients()
             if live(c):
                 hidden(c, range(4, 8))
             if c > 3 and live(c - 2):
@@ -535,7 +540,6 @@ def tile_koopmanae_pa_t_kernel(
                 encode(c - 2)
             if c == 2:
                 regroup_vector(1)
-                place_coefficients()
             if live(c + 1):
                 hidden(c + 1, range(0, 4))
             if live(c - 3):

from contextlib import ExitStack

import concourse.mybir as mybir
from concourse.masks import make_identity

BF16 = mybir.dt.bfloat16
F32 = mybir.dt.float32
I32 = mybir.dt.int32
U32 = mybir.dt.uint32
U8 = mybir.dt.uint8
FP8X4 = mybir.dt.float8_e4m3fn_x4
ACT = mybir.ActivationFunctionType
ALU = mybir.AluOpType

P = 128
PACK = 4
ROWS, D_IN, HID, PAIRS = 4096, 512, 1024, 128
LATENT = 2 * PAIRS
BLOCK = 4
CHUNK = 512
TILES = CHUNK // P
ROW_TILES = ROWS // P
CHUNK_TILES = [2, 4, 4, 4, 4, 4, 4, 2, 2, 2]
N_CHUNKS = len(CHUNK_TILES)
FIRST_TILE = [sum(CHUNK_TILES[:c]) for c in range(N_CHUNKS)]
HID_TILES = HID // P
PASSES2 = HID // (P * PACK)
TERMS = 32
ROW_AMP, ROW_FREQ, ROW_B1, ROW_B2, VEC_ROWS = 32, 33, 34, 42, 44
SCALAR_SHARE = [64 * c for c in range(7)] + [1024] * 3
Z_BANKS = 4

FLOPS = 2 * ROWS * D_IN * HID + 2 * ROWS * HID * LATENT


def regroup(copy, grouped, planes):
    copy(
        out=grouped.rearrange("p (c i) t -> p c t i", i=8),
        in_=planes.rearrange("p t (c i) -> p c t i", i=8),
    )


def quantise(nc, codes, scales, grouped):
    nc.vector.quantize_mx(
        out=codes.bitcast(FP8X4),
        scales=scales,
        in_=grouped.rearrange("p c t -> p (c t)"),
    )


def tile_koopmanae_pa_t_kernel(
    tc, x, delta_t, W_enc1, b_enc1, W_enc2, b_enc2, amplitudes, frequencies, out_0, out_1
):
    nc = tc.nc
    with ExitStack() as ctx:
        keep = ctx.enter_context(tc.tile_pool(name="keep", bufs=1))
        x_pool = ctx.enter_context(tc.tile_pool(name="x_pool", bufs=N_CHUNKS))
        two = ctx.enter_context(tc.tile_pool(name="two", bufs=2))
        three = ctx.enter_context(tc.tile_pool(name="three", bufs=3))
        four = ctx.enter_context(tc.tile_pool(name="four", bufs=4))
        psum_z = ctx.enter_context(tc.psum_pool(name="psum_z", bufs=Z_BANKS))
        psum_enc = ctx.enter_context(tc.psum_pool(name="psum_enc", bufs=2))
        psum_turn = ctx.enter_context(tc.psum_pool(name="psum_turn", bufs=1))
        ctx.enter_context(tc.manual_schedule())

        vec = keep.tile([P, P], BF16)
        nc.vector.memset(vec[:].bitcast(I32), 0)

        def load_vectors():
            nc.sync.dma_start(out=vec[0:ROW_AMP, :], in_=delta_t.rearrange("(t r) -> t r", r=P))
            nc.sync.dma_start(
                out=vec[ROW_AMP:ROW_FREQ, :], in_=amplitudes.rearrange("(o i) -> o i", o=1)
            )
            nc.sync.dma_start(
                out=vec[ROW_FREQ:ROW_B1, :], in_=frequencies.rearrange("(o i) -> o i", o=1)
            )
            nc.sync.dma_start(out=vec[ROW_B1:ROW_B2, :], in_=b_enc1.rearrange("(m p) -> m p", p=P))
            nc.sync.dma_start(out=vec[ROW_B2:VEC_ROWS, :], in_=b_enc2.rearrange("(m p) -> m p", p=P))

        def rows_of(c):
            return slice(P * FIRST_TILE[c], P * (FIRST_TILE[c] + CHUNK_TILES[c]))

        x_sb = {}

        def load_x(c):
            x_sb[c] = x_pool.tile([P, TILES, D_IN], BF16, name="x_sb")
            nc.sync.dma_start(
                out=x_sb[c][:, 0 : CHUNK_TILES[c], :],
                in_=x[rows_of(c), :].rearrange("(a r) k -> r a k", r=P),
            )

        load_x(0)
        W1_HALVES = [slice(0, HID // 2), slice(HID // 2, HID)]
        w1_rows = W_enc1.rearrange("(u q e) c -> q u e c", u=2, e=2)
        w1_raw = []
        for half, cols in enumerate(W1_HALVES):
            raw = keep.tile([P, PACK, HID // 2], BF16, name="w1_raw_%d" % half)
            for u in range(2):
                nc.sync.dma_start(out=raw[:, 2 * u : 2 * u + 2, :], in_=w1_rows[:, u, :, cols])
            w1_raw.append(raw)
            if half == 0:
                load_vectors()
        load_x(1)
        w2_raw = keep.tile([P, HID_TILES, LATENT], BF16)
        nc.sync.dma_start(out=w2_raw[:], in_=W_enc2.rearrange("(m p) f -> p m f", p=P))
        for c in range(2, N_CHUNKS):
            load_x(c)

        counts = keep.tile([P, TERMS - 1], F32)
        nc.gpsimd.iota(
            counts[:],
            pattern=[[1, TERMS - 1]],
            base=1,
            channel_multiplier=0,
            allow_small_or_imprecise_dtypes=True,
        )
        identity = keep.tile([P, P], F32)
        make_identity(nc, identity[:])
        identity_bf = keep.tile([P, P], BF16)
        nc.gpsimd.tensor_copy(out=identity_bf[:], in_=identity[:])

        first = keep.tile([P, 1], F32)
        nc.vector.memset(first[:], 1.0)
        table_choice = keep.tile([P, 1], F32)
        nc.scalar.activation(out=table_choice[:], in_=first[:], func=ACT.Ln)

        coef = keep.tile([P, 2, 4, TERMS], F32)
        blocks = keep.tile([P, 2, TILES, PAIRS], F32)
        nc.gpsimd.memset(blocks[:], 0.0)
        zpow = keep.tile([P, 2, TERMS], F32)
        nc.vector.memset(zpow[:, 0, 0:1], 1.0)
        nc.vector.memset(zpow[:, 1, 0:1], 0.0)
        tpow = keep.tile([P, ROW_TILES, TERMS], F32)
        nc.gpsimd.memset(tpow[:, :, 0:1], 1.0)
        inverses = keep.tile([P, TERMS - 1], F32)
        zeros = keep.tile([P, TERMS - 1], F32)
        inv_fact = keep.tile([P, TERMS], F32)

        def inverse_factorials():
            nc.vector.memset(zeros[:], 0.0)
            nc.vector.memset(inv_fact[:, 0:1], 1.0)
            nc.vector.reciprocal(out=inverses[:], in_=counts[:])
            nc.vector.tensor_tensor_scan(
                out=inv_fact[:, 1:TERMS],
                data0=inverses[:],
                data1=zeros[:],
                initial=1.0,
                op0=ALU.mult,
                op1=ALU.add,
            )

        columns = keep.tile([P, VEC_ROWS], F32)
        b2_all = keep.tile([P, LATENT], F32)

        def spread_vectors():
            turned = psum_z.tile([P, P], BF16, tag="z")
            nc.tensor.transpose(turned[:], vec[:], identity_bf[:])
            nc.vector.tensor_copy(out=columns[:], in_=turned[:, 0:VEC_ROWS])
            spread = psum_z.tile([P, LATENT], F32, tag="z")
            for m in range(2):
                row = ROW_B2 + m
                nc.tensor.matmul(
                    out=spread[:, P * m : P * m + P],
                    lhsT=identity_bf[:, row : row + 1].to_broadcast([P, P]),
                    rhs=vec[:],
                    start=True,
                    stop=True,
                )
            return spread

        def first_power():
            nc.scalar.activation(
                out=zpow[:, 0, 1:2], in_=columns[:, ROW_AMP:ROW_FREQ], func=ACT.Ln
            )
            nc.vector.tensor_copy(out=zpow[:, 1, 1:2], in_=columns[:, ROW_FREQ:ROW_B1])

        by_im = keep.tile([P, 2, TERMS // 2], F32)

        def power_count(m):
            return min(m, TERMS - 1 - m)

        def times_imaginary(m):
            n = power_count(m)
            nc.vector.tensor_scalar(
                out=by_im[:, :, 0:n],
                in0=zpow[:, :, 1 : 1 + n],
                scalar1=zpow[:, 1, m : m + 1],
                scalar2=None,
                op0=ALU.mult,
            )

        def next_powers(m):
            n = power_count(m)
            for part, other, op in ((0, 1, ALU.subtract), (1, 0, ALU.add)):
                nc.vector.scalar_tensor_tensor(
                    out=zpow[:, part, m + 1 : m + 1 + n],
                    in0=zpow[:, part, 1 : 1 + n],
                    scalar=zpow[:, 0, m : m + 1],
                    in1=by_im[:, other, 0:n],
                    op0=ALU.mult,
                    op1=op,
                )

        def coefficients():
            for part in range(2):
                nc.vector.tensor_mul(
                    out=coef[:, part],
                    in0=zpow[:, part, :].unsqueeze(1).to_broadcast([P, 4, TERMS]),
                    in1=inv_fact[:].unsqueeze(1).to_broadcast([P, 4, TERMS]),
                )

        def powers():
            nc.gpsimd.tensor_copy(out=tpow[:, :, 1:2], in_=columns[:, 0:ROW_AMP].unsqueeze(2))
            m = 1
            while m < TERMS - 1:
                n = min(m, TERMS - 1 - m)
                nc.gpsimd.tensor_mul(
                    out=tpow[:, :, m + 1 : m + 1 + n],
                    in0=tpow[:, :, 1 : 1 + n],
                    in1=tpow[:, :, m : m + 1].to_broadcast([P, ROW_TILES, n]),
                )
                m = 2 * m

        rows_of_powers = keep.tile([P, ROW_TILES // TILES, P], F32)

        def place_coefficients():
            bank = psum_turn.tile([P, 2, PAIRS], F32, tag="turn_0")
            for part in range(2):
                nc.tensor.transpose(
                    bank[:, part, :], coef[:, part].rearrange("i a k -> i (a k)"), identity[:]
                )
            for a in range(TILES):
                rows = slice(TERMS * a, TERMS * a + TERMS)
                nc.vector.tensor_copy(out=blocks[rows, :, a, :], in_=bank[rows, :, :])

        def place_powers(half):
            bank = psum_turn.tile([P, TILES, P], F32, tag="turn_%d" % half)
            for g4 in range(TILES):
                g = TILES * half + g4
                nc.tensor.transpose(
                    bank[:, g4, :],
                    tpow[:, TILES * g : TILES * g + TILES, :].rearrange("r t k -> r (t k)"),
                    identity[:],
                )
            nc.vector.tensor_copy(
                out=rows_of_powers[:, TILES * half : TILES * half + TILES, :], in_=bank[:]
            )

        w1_grouped = keep.tile([P, HID, PACK], BF16, align_bytes=64)
        w1_codes = keep.tile([P, HID], U32, align_bytes=64)
        w1_scales = keep.tile([P, HID], U8, align_bytes=64)

        def regroup_w1(half, copy, first_col, last_col):
            grouped = w1_grouped[:, W1_HALVES[half], :]
            cols = slice(first_col, last_col)
            regroup(copy, grouped[:, cols, :], w1_raw[half][:, :, cols])

        def quantise_w1(half):
            cols = W1_HALVES[half]
            quantise(nc, w1_codes[:, cols], w1_scales[:, cols], w1_grouped[:, cols, :])

        w2_grouped = keep.tile([P, PASSES2, LATENT, PACK], BF16, align_bytes=64)
        w2_codes = keep.tile([P, PASSES2, LATENT], U32, align_bytes=64)
        w2_scales = keep.tile([P, PASSES2, LATENT], U8, align_bytes=64)

        def regroup_w2(copy):
            for g in range(PASSES2):
                planes = w2_raw[:, PACK * g : PACK * g + PACK, :]
                regroup(copy, w2_grouped[:, g], planes)

        def quantise_w2():
            quantise(
                nc,
                w2_codes[:].rearrange("p g f -> p (g f)"),
                w2_scales[:].rearrange("p g f -> p (g f)"),
                w2_grouped[:].rearrange("p g f t -> p (g f) t"),
            )

        x_banks, x_grouped, x_codes, x_scales = {}, {}, {}, {}
        h_planes, h_grouped, h_codes, h_scales = {}, {}, {}, {}
        turn_factors = {}
        enc_banks, enc, straight, crossed = {}, {}, {}, {}

        def halves(c):
            return range(CHUNK_TILES[c] // 2)

        def out_rows(out, c):
            return out[rows_of(c), :].rearrange("(a r) f -> r a f", r=P)

        bank_of = {
            (1, 0): (psum_enc, "enc_bank"),
            (1, 1): (psum_enc, "enc_bank"),
            (2, 0): (psum_turn, "turn_0"),
            (2, 1): (psum_turn, "turn_1"),
            (3, 0): (psum_enc, "enc_bank"),
            (3, 1): (psum_enc, "enc_bank"),
        }

        def transpose_x(c, half):
            words = x_sb[c][:].bitcast(F32)
            pool, tag = bank_of.get((c, half), (psum_z, "z"))
            bank = pool.tile([P, 2, 2, P], F32, tag=tag)
            for a2 in range(2):
                for u in range(2):
                    nc.tensor.transpose(
                        bank[:, u, a2, :], words[:, 2 * half + a2, P * u : P * u + P], identity[:]
                    )
            x_banks[c, half] = bank

        def copy_x(c, half, copy):
            if half == 0:
                x_grouped[c] = two.tile([P, CHUNK, PACK], BF16, name="x_grouped", align_bytes=64)
            as_words = x_grouped[c][:].bitcast(F32)
            copy(
                out=as_words[:, 2 * P * half : 2 * P * half + 2 * P, :],
                in_=x_banks[c, half][:].rearrange("q u a r -> q (a r) u"),
            )

        def quantise_x(c):
            x_codes[c] = three.tile([P, CHUNK], U32, name="x_codes", align_bytes=64)
            x_scales[c] = three.tile([P, CHUNK], U8, name="x_scales", align_bytes=64)
            n = P * CHUNK_TILES[c]
            quantise(nc, x_codes[c][:, 0:n], x_scales[c][:, 0:n], x_grouped[c][:, 0:n, :])

        def hidden(c, tiles):
            n = P * CHUNK_TILES[c]
            if c not in h_planes:
                h_planes[c] = three.tile([P, PACK, PASSES2, n], BF16, name="h_planes")
            for m in tiles:
                units = slice(P * m, P * m + P)
                z = psum_z.tile([P, CHUNK], F32, tag="z")
                nc.tensor.matmul_mx(
                    out=z[:, 0:n],
                    lhsT=w1_codes[:, units].bitcast(FP8X4),
                    lhsT_scale=w1_scales[:, units],
                    rhs=x_codes[c][:, 0:n].bitcast(FP8X4),
                    rhs_scale=x_scales[c][:, 0:n],
                    start=True,
                    stop=True,
                )
                nc.scalar.activation(
                    out=h_planes[c][:, m % PACK, m // PACK, :],
                    in_=z[:, 0:n],
                    func=ACT.Tanh,
                    bias=columns[:, ROW_B1 + m : ROW_B1 + m + 1],
                )

        def make_factor(c, part):
            bank = psum_turn.tile([P, TILES, PAIRS], F32, tag="turn_%d" % part)
            done = 0
            while done < CHUNK_TILES[c]:
                g, a = divmod(FIRST_TILE[c] + done, TILES)
                n = min(TILES - a, CHUNK_TILES[c] - done)
                nc.tensor.matmul(
                    out=bank[:, done : done + n, :].rearrange("r a i -> r (a i)"),
                    lhsT=rows_of_powers[:, g, :],
                    rhs=blocks[:, part, a : a + n, :].rearrange("k a i -> k (a i)"),
                    start=True,
                    stop=True,
                )
                done += n
            turn_factors[c, part] = bank

        def regroup_h(c, copy, first_word, last_word):
            if c not in h_grouped:
                h_grouped[c] = two.tile(
                    [P, PASSES2 * P * CHUNK_TILES[c], PACK], BF16, name="h_grouped", align_bytes=64
                )
            if first_word == last_word:
                return
            words = slice(first_word, last_word)
            planes = h_planes[c][:].rearrange("p t g r -> p t (g r)")
            regroup(copy, h_grouped[c][:, words, :], planes[:, :, words])

        def vector_words(c):
            return (PASSES2 * CHUNK - SCALAR_SHARE[c]) * CHUNK_TILES[c] // TILES

        def regroup_vector(c):
            regroup_h(c, nc.vector.tensor_copy, 0, vector_words(c))

        def regroup_scalar(c):
            regroup_h(c, nc.scalar.copy, vector_words(c), PASSES2 * P * CHUNK_TILES[c])

        def quantise_h(c):
            words = PASSES2 * P * CHUNK_TILES[c]
            h_codes[c] = two.tile([P, words], U32, name="h_codes", align_bytes=64)
            h_scales[c] = two.tile([P, words], U8, name="h_scales", align_bytes=64)
            quantise(nc, h_codes[c][:], h_scales[c][:], h_grouped[c][:])

        def encode(c):
            for half in halves(c):
                bank = psum_enc.tile([P, 2, LATENT], F32, tag="enc_bank")
                for a2 in range(2):
                    for g in range(PASSES2):
                        word = P * (CHUNK_TILES[c] * g + 2 * half + a2)
                        words = slice(word, word + P)
                        nc.tensor.matmul_mx(
                            out=bank[:, a2, :],
                            lhsT=h_codes[c][:, words].bitcast(FP8X4),
                            lhsT_scale=h_scales[c][:, words],
                            rhs=w2_codes[:, g, :].bitcast(FP8X4),
                            rhs_scale=w2_scales[:, g, :],
                            start=(g == 0),
                            stop=(g == PASSES2 - 1),
                        )
                enc_banks[c, half] = bank

        def add_bias2(c):
            enc[c] = three.tile([P, TILES, LATENT], F32, name="enc")
            for half in halves(c):
                nc.vector.tensor_add(
                    out=enc[c][:, 2 * half : 2 * half + 2, :],
                    in0=enc_banks[c, half][:],
                    in1=b2_all[:].unsqueeze(1).to_broadcast([P, 2, LATENT]),
                )
            nc.sync.dma_start(out=out_rows(out_1, c), in_=enc[c][:, 0 : CHUNK_TILES[c], :])

        def pairs_of(c):
            return enc[c][:].rearrange("p a (i h) -> p (a i) h", h=2)

        def turn_straight(c):
            n = CHUNK_TILES[c] * PAIRS
            cos_grown = turn_factors[c, 0][:].rearrange("p a i -> p (a i)")[:, 0:n]
            straight[c] = three.tile([P, TILES * PAIRS, 2], F32, name="straight")
            nc.vector.tensor_mul(
                out=straight[c][:, 0:n, :],
                in0=pairs_of(c)[:, 0:n, :],
                in1=cos_grown.unsqueeze(2).to_broadcast([P, n, 2]),
            )

        def turn_crossed(c):
            n = CHUNK_TILES[c] * PAIRS
            pairs = pairs_of(c)[:, 0:n, :].rearrange("p (b i) h -> p b i h", i=BLOCK)
            sin_grown = turn_factors[c, 1][:].rearrange("p a i -> p (a i)")[:, 0:n]
            sin_grown = sin_grown.rearrange("p (b i) -> p b i", i=BLOCK)
            crossed[c] = three.tile([P, TILES * PAIRS // BLOCK, 2, BLOCK], F32, name="crossed")
            nc.vector.scalar_tensor_tensor(
                out=crossed[c][:, 0 : n // BLOCK, 0, :],
                in0=pairs[:, :, :, 1],
                scalar=-1.0,
                in1=sin_grown,
                op0=ALU.mult,
                op1=ALU.mult,
            )
            nc.vector.tensor_mul(
                out=crossed[c][:, 0 : n // BLOCK, 1, :], in0=pairs[:, :, :, 0], in1=sin_grown
            )

        waited_for = keep.tile([P, 1], U32)

        def turn_sum(c, engine):
            n = CHUNK_TILES[c] * PAIRS
            pred = four.tile([P, TILES * PAIRS, 2], F32)
            engine.tensor_add(
                out=pred[:, 0:n, :].rearrange("p (b i) h -> p b h i", i=BLOCK),
                in0=straight[c][:, 0:n, :].rearrange("p (b i) h -> p b h i", i=BLOCK),
                in1=crossed[c][:, 0 : n // BLOCK],
            )
            nc.sync.dma_start(
                out=out_rows(out_0, c),
                in_=pred[:, 0:n, :].rearrange("p (a i) h -> p a (i h)", i=PAIRS),
            )

        def hold_sum(c):
            nc.gpsimd.tensor_copy(out=waited_for[:], in_=h_codes[c][:, 0:1])

        def prepare_x(c, copy):
            for half in halves(c):
                transpose_x(c, half)
            for half in halves(c):
                copy_x(c, half, copy)

        inverse_factorials()
        prepare_x(0, nc.vector.tensor_copy)
        spread = spread_vectors()
        regroup_w1(0, nc.vector.tensor_copy, 0, 320)
        regroup_w1(0, nc.scalar.copy, 320, 512)
        powers()
        first_power()
        nc.scalar.activation(out=table_choice[:], in_=first[:], func=ACT.Tanh)
        quantise_x(0)
        quantise_w1(0)
        regroup_w1(1, nc.scalar.copy, 320, 512)
        hidden(0, range(0, 4))
        regroup_w1(1, nc.vector.tensor_copy, 0, 320)
        times_imaginary(1)
        nc.vector.tensor_copy(out=b2_all[:], in_=spread[:])
        quantise_w1(1)
        next_powers(1)
        prepare_x(1, nc.vector.tensor_copy)
        times_imaginary(2)
        hidden(0, range(4, 8))
        regroup_scalar(0)
        quantise_x(1)
        next_powers(2)
        prepare_x(2, nc.vector.tensor_copy)
        hidden(1, range(0, 4))
        times_imaginary(4)
        quantise_x(2)
        next_powers(4)
        regroup_w2(nc.vector.tensor_copy)
        times_imaginary(8)
        prepare_x(3, nc.vector.tensor_copy)
        hidden(1, range(4, 8))
        regroup_scalar(1)
        next_powers(8)
        place_powers(0)
        place_powers(1)
        times_imaginary(16)
        quantise_w2()
        next_powers(16)
        hidden(2, range(0, 4))
        quantise_x(3)
        coefficients()
        regroup_vector(0)

        def live(c):
            return 0 <= c < N_CHUNKS

        for c in range(2, N_CHUNKS + 3):
            if live(c - 3):
                make_factor(c - 3, 0)
            if live(c + 2):
                prepare_x(c + 2, nc.scalar.copy)
            if live(c - 3):
                make_factor(c - 3, 1)
            if c == 2:
                place_coefficients()
            if live(c):
                hidden(c, range(4, 8))
            if c > 3 and live(c - 2):
                regroup_vector(c - 2)
            if c > 2 and live(c + 1):
                quantise_x(c + 1)
            if live(c - 2):
                quantise_h(c - 2)
            if live(c):
                regroup_scalar(c)
            if live(c - 2):
                encode(c - 2)
            if c == 2:
                regroup_vector(1)
            if live(c + 1):
                hidden(c + 1, range(0, 4))
            if live(c - 3):
                turn_straight(c - 3)
                turn_crossed(c - 3)
            if live(c - 2):
                add_bias2(c - 2)
            if live(c - 4) and c - 4 < N_CHUNKS - 2:
                if live(c - 2):
                    hold_sum(c - 2)
                turn_sum(c - 4, nc.gpsimd)
            if N_CHUNKS - 2 <= c - 3 < N_CHUNKS:
                turn_sum(c - 3, nc.vector)
